import numpy as np
import ml_dtypes


def mxq(x, axis, fmt="e4m3"):
    dtype, down = {"e4m3": (ml_dtypes.float8_e4m3fn, 7), "e5m2": (ml_dtypes.float8_e5m2, 14)}[fmt]
    v = np.moveaxis(np.asarray(x, np.float32).astype(ml_dtypes.bfloat16).astype(np.float64), axis, -1)
    blocks = v.reshape(v.shape[:-1] + (-1, 32))
    amax = np.abs(blocks).max(-1, keepdims=True)
    byte = np.maximum(np.where(amax > 0, np.frexp(amax)[1] - 1 + 127, 0) - down, 1)
    scale = np.exp2(byte - 127.0)
    codes = (blocks / scale).astype(np.float32).astype(dtype).astype(np.float64)
    return np.moveaxis((codes * scale).reshape(v.shape), -1, axis)


WIDE = False


def mx_kscale(k):
    if not WIDE:
        return np.ones(k)
    levels = np.array([10, -10, 5, -5, 0])
    a = np.random.permutation(np.resize(levels, k // 512 * 4)).reshape(k // 512, 4)
    idx = np.arange(k)
    return np.exp2(a[idx // 512, idx % 128 // 32])


BF16 = ml_dtypes.bfloat16


def bf(x):
    return np.asarray(x, np.float32).astype(BF16)


def f64(x):
    return np.asarray(x).astype(np.float64)


B, P, DIN, COND, HID, HA, HB, HC, OUT = 4, 1024, 3, 48, 1024, 512, 1024, 256, 257
N = B * P
INV_SQRT2 = np.sqrt(0.5)


def softplus_beta100(v):
    z = 100.0 * v
    return (np.maximum(z, 0.0) + np.log(1.0 + np.exp(-np.abs(z)))) * 0.01


def setup_inputs():
    s = mx_kscale(HA)
    return {"h3": bf(softplus_beta100(0.03 + 0.016 * np.random.standard_normal((N, HA - DIN))) * s[:HA - DIN]),
            "x_in": bf(np.random.uniform(-1.0, 1.0, (N, DIN)) * s[HA - DIN:]),
            "W4": bf(np.random.standard_normal((HB, HA)) * 0.42 / np.sqrt(HA) / s[None, :]),
            "b4": bf(0.03 + 0.005 * np.random.standard_normal(HB)),
            "W5": bf(np.random.standard_normal((HC, HB)) * 2.6 / np.sqrt(HB)),
            "b5": bf(np.random.standard_normal(HC) * 0.04)}


def reference(h3, x_in, W4, b4, W5, b5):
    x = np.concatenate([f64(h3), f64(x_in)], axis=-1) * INV_SQRT2
    h4 = softplus_beta100((mxq(x, 1, "e4m3") @ mxq(f64(W4), 1, "e4m3").T) + f64(b4))
    return softplus_beta100((mxq(h4, 1, "e4m3") @ mxq(f64(W5), 1, "e4m3").T) + f64(b5))

@@ -1,0 +1,409 @@
+import math
+from contextlib import ExitStack
+
+import concourse.mybir as mybir
+from concourse.masks import make_identity
+
+F32 = mybir.dt.float32
+BF16 = mybir.dt.bfloat16
+U32 = mybir.dt.uint32
+U8 = mybir.dt.uint8
+FP8X4 = mybir.dt.float8_e4m3fn_x4
+ALU = mybir.AluOpType
+FN = mybir.ActivationFunctionType
+
+P = 128
+N_TOK, HA, HB, HC, DIN = 4096, 512, 1024, 256, 3
+FLOPS = 2 * N_TOK * HA * HB + 2 * N_TOK * HB * HC
+NG = N_TOK // P
+NQ = 8
+CHUNKS = ((0, 1, 2), (3, 4, 5), (6, 7))
+DELTA = 2.0 ** -62
+BUFS = {"pt": 2, "pa": 2, "pd": 2, "po": 2, "xr": 1, "xg": 1, "S": 6, "Wg": 6, "Ag": 2, "Hc": 2, "w2": 3, "s2": 4}
+TABLE_LOAD = 1300
+HOP = 60
+
+
+def plan(ops, queues, emit):
+    end = {}
+    free = {}
+    ptr = {}
+    uses = {}
+    slot = {}
+    state = {"fn": None}
+    for e in queues:
+        free[e] = 0
+        ptr[e] = [0 for c in queues[e]]
+    total = sum(len(c) for e in queues for c in queues[e])
+    assert total == len(ops), (total, len(ops))
+
+    def ready(e, name):
+        op = ops[name]
+        t = free[e]
+        deps = list(op["deps"])
+        if op["ring"] is not None:
+            tag = op["ring"][0]
+            used = uses.get(tag, [])
+            if len(used) >= BUFS[tag]:
+                deps.extend(used[len(used) - BUFS[tag]])
+        for d in deps:
+            if isinstance(d, int):
+                t = max(t, d)
+            elif d not in end:
+                return None
+            else:
+                t = max(t, end[d] + (0 if ops[d]["eng"] == e else HOP))
+        return t
+
+    done = 0
+    while done < total:
+        best = None
+        for e in queues:
+            for ci, c in enumerate(queues[e]):
+                if ptr[e][ci] >= len(c):
+                    continue
+                t = ready(e, c[ptr[e][ci]])
+                if t is None:
+                    continue
+                key = (t, ci)
+                if best is None or key < best[0]:
+                    best = (key, e, ci)
+        assert best is not None, "the plan is stuck"
+        key, e, ci = best
+        name = queues[e][ci][ptr[e][ci]]
+        op = ops[name]
+        t = key[0]
+        if op["fn"] is not None and op["fn"] != state["fn"]:
+            t = max(t, free[e] + TABLE_LOAD)
+            state["fn"] = op["fn"]
+        if op["ring"] is not None:
+            tag = op["ring"][0]
+            used = uses.get(tag, [])
+            slot[name] = len(used) % BUFS[tag]
+            uses[tag] = used + [op["ring"][1]]
+        end[name] = t + op["cost"]
+        free[e] = end[name]
+        ptr[e][ci] += 1
+        done += 1
+        emit(name, slot)
+
+
+def tile_implicitnet_pa_t_kernel(tc, h3, x_in, W4, b4, W5, b5, out):
+    nc = tc.nc
+    h3v = h3.rearrange("(p g) k -> p g k", g=NG)
+    outv = out.rearrange("(p g) n -> p g n", g=NG)
+    cut = 496
+
+    with ExitStack() as ctx:
+        keep = ctx.enter_context(tc.tile_pool(name="keep", bufs=1))
+        psum = ctx.enter_context(tc.psum_pool(name="psum", bufs=1))
+        ctx.enter_context(tc.manual_schedule())
+
+        def sb(shape, dt, name, n=None):
+            if n is None:
+                return keep.tile(shape, dt, name=name, align_bytes=64)
+            return [keep.tile(shape, dt, name="%s%d" % (name, i), align_bytes=64) for i in range(n)]
+
+        bank = {}
+        for tag in ("pt", "pa", "pd", "po"):
+            bank[tag] = [psum.tile([P, 512], F32, name="%s%d" % (tag, i)) for i in range(BUFS[tag])]
+
+        ident = sb([P, P], F32, "ident")
+        dl = sb([P, 1], F32, "dl")
+        warm = sb([P, 1], F32, "warm")
+        b4b = sb([P, 8], BF16, "b4b")
+        b4f = sb([P, 8], F32, "b4f")
+        nb4 = sb([P, 8], F32, "nb4")
+        b5bc = sb([P, HC], BF16, "b5bc")
+        tail13 = sb([P, NG, 16], BF16, "tail13")
+        xin = sb([P, NG * DIN], BF16, "xin")
+        X = sb([P, 4, HA], BF16, "X", NQ)
+        xr = sb([P, 2048], BF16, "xr", BUFS["xr"])
+        xg = sb([P, 2048], BF16, "xg", BUFS["xg"])
+        xc = sb([P, 512], U32, "xc", NQ)
+        xs = sb([P, 512], U8, "xs", NQ)
+        w4sb = sb([P, 8 * HA], BF16, "w4sb")
+        w4g = sb([P, 8 * HA], BF16, "w4g")
+        w4c = sb([P, HB], U32, "w4c")
+        w4s = sb([P, HB], U8, "w4s")
+        w5sb = sb([P, 2 * HB], BF16, "w5sb")
+        w5g = sb([P, 2 * HB], BF16, "w5g")
+        w5c = sb([P, 512], U32, "w5c")
+        w5s = sb([P, 512], U8, "w5s")
+        S = sb([P, 4, 512], F32, "S", BUFS["S"])
+        Wg = sb([P, 2048], BF16, "Wg", BUFS["Wg"])
+        Ag = sb([P, 2048], BF16, "Ag", BUFS["Ag"])
+        Hc = sb([P, 2, 512], U32, "Hc", BUFS["Hc"])
+        Hs = sb([P, 2, 512], U8, "Hs", BUFS["Hc"])
+        w2 = sb([P, 1024], F32, "w2", BUFS["w2"])
+        s2 = sb([P, 1024], F32, "s2", BUFS["s2"])
+
+        nc.vector.memset(dl[:], DELTA)
+        nc.scalar.activation(out=warm[:], in_=dl[:], func=FN.Sigmoid)
+        make_identity(nc, ident[:])
+        nc.scalar.dma_start(out=xin[:], in_=x_in.rearrange("(p g) c -> p (g c)", g=NG))
+        for a in range(4):
+            nc.scalar.dma_start(out=tail13[:, 8 * a : 8 * a + 8, 0:13], in_=h3v[:, 8 * a : 8 * a + 8, cut : HA - DIN])
+        nc.gpsimd.dma_start(out=b4b[:].rearrange("p (g t) -> p g t", g=2), in_=b4.rearrange("(g p t) -> p g t", g=2, t=4))
+        nc.gpsimd.dma_start(out=b5bc[:], in_=b5.partition_broadcast(P))
+
+        ops = {}
+
+        def op(name, eng, cost, deps, run, ring=None, fn=None):
+            ops[name] = {"eng": eng, "cost": cost, "deps": deps, "ring": ring, "fn": fn, "run": run}
+
+        def words(t):
+            return t[:].bitcast(F32)
+
+        def mx(o, lw, ls, rw, rs, start, stop):
+            nc.tensor.matmul_mx(out=o, lhsT=lw.bitcast(FP8X4), lhsT_scale=ls, rhs=rw.bitcast(FP8X4), rhs_scale=rs, start=start, stop=stop)
+
+        def ld_x(q):
+            return lambda sl: nc.sync.dma_start(out=X[q][:, :, 0:cut], in_=h3v[:, 4 * q : 4 * q + 4, 0:cut])
+
+        def ld_w4(h):
+            return lambda sl: nc.sync.dma_start(
+                out=w4sb[:, 2048 * h : 2048 * h + 2048], in_=W4.rearrange("(g m t) k -> m g (t k)", g=2, t=4)[:, h, :]
+            )
+
+        def ld_w5(sl):
+            nc.sync.dma_start(out=w5sb[:].rearrange("p (a k) -> p a k", a=2), in_=W5.rearrange("(a n) k -> n a k", a=2))
+
+        op("LX0", "SP", 3000, [], ld_x(0))
+        op("LW0", "SP", 1000, [], ld_w4(0))
+        op("LW1", "SP", 1000, [], ld_w4(1))
+        for q in range(1, NQ):
+            op("LX%d" % q, "SP", 1000, [], ld_x(q))
+        op("LW5", "SP", 1000, [], ld_w5)
+
+        def run_b4(sl):
+            nc.vector.tensor_copy(out=b4f[:], in_=b4b[:])
+            nc.vector.tensor_scalar(out=nb4[:], in0=b4b[:], scalar1=-100.0, scalar2=None, op0=ALU.mult)
+
+        op("B4", "DVE", 150, [3000], run_b4)
+
+        def w4t(k):
+            def run(sl):
+                pt = bank["pt"][sl["W4T%d" % k]]
+                for jj in range(2):
+                    for u in range(2):
+                        j = 2 * k + jj
+                        nc.tensor.transpose(pt[:, 256 * jj + 128 * u : 256 * jj + 128 * u + 128], words(w4sb)[:, 256 * j + 128 * u : 256 * j + 128 * u + 128], ident[:])
+            return run
+
+        def w4e(k):
+            def run(sl):
+                pt = bank["pt"][sl["W4T%d" % k]]
+                nc.scalar.copy(
+                    out=words(w4g).rearrange("p (j m u) -> p j m u", j=8, u=2)[:, 2 * k : 2 * k + 2],
+                    in_=pt[:].rearrange("p (j u m) -> p j m u", j=2, u=2),
+                )
+            return run
+
+        def w4q(h):
+            return lambda sl: nc.vector.quantize_mx(
+                out=w4c[:, 512 * h : 512 * h + 512].bitcast(FP8X4), scales=w4s[:, 512 * h : 512 * h + 512], in_=w4g[:, 2048 * h : 2048 * h + 2048]
+            )
+
+        for k in range(4):
+            op("W4T%d" % k, "PE", 260, ["LW%d" % (k // 2)], w4t(k), ring=("pt", ["W4E%d" % k]))
+            op("W4E%d" % k, "ACT", 450, ["W4T%d" % k], w4e(k))
+        for h in range(2):
+            op("W4Q%d" % h, "DVE", 470, ["W4E%d" % (2 * h), "W4E%d" % (2 * h + 1)], w4q(h))
+
+        def w5t(g):
+            def run(sl):
+                pt = bank["pt"][sl["W5T%d" % g]]
+                for a in range(2):
+                    for u in range(2):
+                        lo = 512 * a + 256 * g + u
+                        nc.tensor.transpose(pt[:, 256 * a + 128 * u : 256 * a + 128 * u + 128], words(w5sb)[:, lo : lo + 255 : 2], ident[:])
+            return run
+
+        def w5e(g):
+            def run(sl):
+                pt = bank["pt"][sl["W5T%d" % g]]
+                nc.vector.tensor_copy(
+                    out=words(w5g).rearrange("p (g a n u) -> p g a n u", g=2, a=2, u=2)[:, g],
+                    in_=pt[:].rearrange("p (a u n) -> p a n u", a=2, u=2),
+                )
+            return run
+
+        for g in range(2):
+            op("W5T%d" % g, "PE", 420, ["LW5"], w5t(g), ring=("pt", ["W5E%d" % g]))
+            op("W5E%d" % g, "DVE", 450, ["W5T%d" % g], w5e(g))
+        op("W5Q", "DVE", 470, ["W5E0", "W5E1"], lambda sl: nc.vector.quantize_mx(out=w5c[:].bitcast(FP8X4), scales=w5s[:], in_=w5g[:]))
+
+        def xcat(q):
+            def run(sl):
+                nc.vector.tensor_copy(out=X[q][:, :, cut : HA - DIN], in_=tail13[:, 4 * q : 4 * q + 4, 0:13])
+                nc.vector.tensor_copy(out=X[q][:, :, HA - DIN : HA], in_=xin[:].rearrange("p (g c) -> p g c", c=DIN)[:, 4 * q : 4 * q + 4, :])
+            return run
+
+        def xt(q, b):
+            def run(sl):
+                pt = bank["pt"][sl["T%d.%d" % (q, b)]]
+                xw = X[q][:].rearrange("p g k -> p (g k)").bitcast(F32)
+                for ii in range(2):
+                    for u in range(2):
+                        lo = 256 * (2 * b + ii) + 128 * u
+                        nc.tensor.transpose(pt[:, 256 * ii + 128 * u : 256 * ii + 128 * u + 128], xw[:, lo : lo + 128], ident[:])
+            return run
+
+        def xe(q, b):
+            def run(sl):
+                pt = bank["pt"][sl["T%d.%d" % (q, b)]]
+                nc.vector.tensor_copy(
+                    out=words(xr[sl["XE%d.0" % q]]).rearrange("p (i r u) -> p i r u", i=4, u=2)[:, 2 * b : 2 * b + 2],
+                    in_=pt[:].rearrange("p (i u r) -> p i r u", i=2, u=2),
+                )
+            return run
+
+        def xscale(q):
+            return lambda sl: nc.vector.tensor_scalar(
+                out=xg[sl["XS%d" % q]][:], in0=xr[sl["XE%d.0" % q]][:], scalar1=math.sqrt(0.5), scalar2=None, op0=ALU.mult
+            )
+
+        def xquant(q):
+            return lambda sl: nc.vector.quantize_mx(out=xc[q][:].bitcast(FP8X4), scales=xs[q][:], in_=xg[sl["XS%d" % q]][:])
+
+        def l1a(q, j):
+            return lambda sl: mx(bank["pa"][sl["A%d.%d" % (q, j)]][:], w4c[:, 128 * j : 128 * j + 128], w4s[:, 128 * j : 128 * j + 128], xc[q][:], xs[q][:], True, True)
+
+        def sig1(q, j):
+            return lambda sl: nc.scalar.activation(
+                out=S[sl["S1_%d.%d" % (q, 4 * (j // 4))]][:, j % 4, :], in_=bank["pa"][sl["A%d.%d" % (q, j)]][:], func=FN.Sigmoid, bias=nb4[:, j : j + 1], scale=-100.0
+            )
+
+        def l1d(q, k):
+            def run(sl):
+                pd = bank["pd"][sl["D%d.%d" % (q, k)]]
+                i, g = k // 2, k % 2
+                for t in range(4):
+                    j = 4 * g + t
+                    mx(pd[:, 128 * t : 128 * t + 128], w4c[:, 128 * j : 128 * j + 128], w4s[:, 128 * j : 128 * j + 128], xc[q][:, 128 * i : 128 * i + 128], xs[q][:, 128 * i : 128 * i + 128], True, True)
+            return run
+
+        def wguard(q, k):
+            def run(sl):
+                i, g = k // 2, k % 2
+                nc.vector.tensor_tensor(
+                    out=Wg[sl["WG%d.%d" % (q, g)]][:].rearrange("p (i r t) -> p i r t", i=4, t=4)[:, i],
+                    in0=bank["pd"][sl["D%d.%d" % (q, k)]][:].rearrange("p (t r) -> p r t", t=4),
+                    in1=b4f[:, 4 * g : 4 * g + 4].unsqueeze(1).to_broadcast([P, P, 4]),
+                    op=ALU.add,
+                )
+            return run
+
+        def ln1(q, g):
+            def run(sl):
+                s = S[sl["S1_%d.%d" % (q, 4 * g)]][:].rearrange("p t x -> p (t x)")
+                nc.scalar.activation(out=s, in_=s, func=FN.Ln, bias=dl[:], scale=1.0)
+            return run
+
+        def pscale(q, g):
+            return lambda sl: nc.gpsimd.tensor_scalar(
+                out=Ag[sl["PA%d.%d" % (q, g)]][:].rearrange("p (x t) -> p x t", t=4),
+                in0=S[sl["S1_%d.%d" % (q, 4 * g)]][:].rearrange("p t x -> p x t"),
+                scalar1=-0.01, scalar2=0.0, op0=ALU.mult, op1=ALU.add,
+            )
+
+        def hmax(q, g):
+            def run(sl):
+                a = Ag[sl["PA%d.%d" % (q, g)]]
+                nc.vector.tensor_tensor(out=a[:], in0=a[:], in1=Wg[sl["WG%d.%d" % (q, g)]][:], op=ALU.max)
+            return run
+
+        def hquant(q, g):
+            return lambda sl: nc.vector.quantize_mx(
+                out=Hc[sl["HQ%d.0" % q]][:, g, :].bitcast(FP8X4), scales=Hs[sl["HQ%d.0" % q]][:, g, :], in_=Ag[sl["PA%d.%d" % (q, g)]][:]
+            )
+
+        def l2(q, b):
+            def run(sl):
+                po = bank["po"][sl["O%d.%d" % (q, b)]]
+                hc, hs = Hc[sl["HQ%d.0" % q]], Hs[sl["HQ%d.0" % q]]
+                for ii in range(2):
+                    i = 2 * b + ii
+                    for g in range(2):
+                        mx(po[:, 256 * ii : 256 * ii + 256], hc[:, g, 128 * i : 128 * i + 128], hs[:, g, 128 * i : 128 * i + 128], w5c[:, 256 * g : 256 * g + 256], w5s[:, 256 * g : 256 * g + 256], g == 0, g == 1)
+            return run
+
+        def oe(q, b):
+            return lambda sl: nc.vector.tensor_tensor(
+                out=w2[sl["OE%d.0" % q]][:].rearrange("p (i n) -> p i n", i=4)[:, 2 * b : 2 * b + 2],
+                in0=bank["po"][sl["O%d.%d" % (q, b)]][:].rearrange("p (i n) -> p i n", i=2),
+                in1=b5bc[:].unsqueeze(1).to_broadcast([P, 2, HC]),
+                op=ALU.add,
+            )
+
+        def sig2(q):
+            return lambda sl: nc.scalar.activation(out=s2[sl["S2_%d" % q]][:], in_=w2[sl["OE%d.0" % q]][:], func=FN.Sigmoid, scale=-100.0)
+
+        def ln2(q):
+            return lambda sl: nc.scalar.activation(out=s2[sl["S2_%d" % q]][:], in_=s2[sl["S2_%d" % q]][:], func=FN.Ln, bias=dl[:], scale=1.0)
+
+        def fin2(q):
+            return lambda sl: nc.vector.scalar_tensor_tensor(
+                out=s2[sl["S2_%d" % q]][:], in0=s2[sl["S2_%d" % q]][:], scalar=-0.01, in1=w2[sl["OE%d.0" % q]][:], op0=ALU.mult, op1=ALU.max
+            )
+
+        def store(q):
+            return lambda sl: nc.sync.dma_start(out=outv[:, 4 * q : 4 * q + 4, :], in_=s2[sl["S2_%d" % q]][:].rearrange("p (i n) -> p i n", i=4))
+
+        for q in range(NQ):
+            op("XC%d" % q, "DVE", 150, ["LX%d" % q, 3500 + 500 * (q // 2)], xcat(q))
+            for b in range(2):
+                op("T%d.%d" % (q, b), "PE", 260, ["XC%d" % q], xt(q, b), ring=("pt", ["XE%d.%d" % (q, b)]))
+                op("XE%d.%d" % (q, b), "DVE", 450, ["T%d.%d" % (q, b)], xe(q, b), ring=("xr", ["XS%d" % q]) if b == 0 else None)
+            op("XS%d" % q, "DVE", 450, ["XE%d.0" % q, "XE%d.1" % q], xscale(q), ring=("xg", ["XQ%d" % q]))
+            op("XQ%d" % q, "DVE", 470, ["XS%d" % q], xquant(q))
+            for j in range(8):
+                op("A%d.%d" % (q, j), "PE", 220, ["XQ%d" % q, "W4Q%d" % (j // 4)], l1a(q, j), ring=("pa", ["S1_%d.%d" % (q, j)]))
+                op("S1_%d.%d" % (q, j), "ACT", 472, ["A%d.%d" % (q, j), "B4"], sig1(q, j), ring=("S", ["PA%d.%d" % (q, j // 4)]) if j % 4 == 0 else None, fn="sig")
+            for k in range(8):
+                op("D%d.%d" % (q, k), "PE", 246, ["XQ%d" % q, "W4Q%d" % (k % 2)], l1d(q, k), ring=("pd", ["WG%d.%d" % (q, k)]))
+                op("WG%d.%d" % (q, k), "DVE", 480, ["D%d.%d" % (q, k), "B4"], wguard(q, k), ring=("Wg", ["MX%d.%d" % (q, k)]) if k < 2 else None)
+            for g in range(2):
+                op("L1_%d.%d" % (q, g), "ACT", 1725, ["S1_%d.%d" % (q, 4 * g + t) for t in range(4)], ln1(q, g), fn="ln")
+                op("PA%d.%d" % (q, g), "POOL", 2150, ["L1_%d.%d" % (q, g)], pscale(q, g), ring=("Ag", ["HQ%d.%d" % (q, g)]))
+                op("MX%d.%d" % (q, g), "DVE", 870, ["PA%d.%d" % (q, g)] + ["WG%d.%d" % (q, 2 * i + g) for i in range(4)], hmax(q, g))
+                op("HQ%d.%d" % (q, g), "DVE", 470, ["MX%d.%d" % (q, g)], hquant(q, g), ring=("Hc", ["O%d.0" % q, "O%d.1" % q]) if g == 0 else None)
+            for b in range(2):
+                op("O%d.%d" % (q, b), "PE", 444, ["HQ%d.0" % q, "HQ%d.1" % q, "W5Q"], l2(q, b), ring=("po", ["OE%d.%d" % (q, b)]))
+                op("OE%d.%d" % (q, b), "DVE", 480, ["O%d.%d" % (q, b)], oe(q, b), ring=("w2", ["F2_%d" % q]) if b == 0 else None)
+            op("S2_%d" % q, "ACT", 872, ["OE%d.0" % q, "OE%d.1" % q], sig2(q), ring=("s2", ["ST%d" % q]), fn="sig")
+            op("L2_%d" % q, "ACT", 872, ["S2_%d" % q], ln2(q), fn="ln")
+            op("F2_%d" % q, "DVE", 900, ["L2_%d" % q], fin2(q))
+            op("ST%d" % q, "SP", 2200, ["F2_%d" % q], store(q))
+
+        quads = [q for c in CHUNKS for q in c]
+        act = ["W4E%d" % k for k in range(4)]
+        for ci, c in enumerate(CHUNKS):
+            prev = CHUNKS[ci - 1] if ci > 0 else ()
+            act += ["S1_%d.%d" % (q, j) for q in c for j in range(8)] + ["S2_%d" % q for q in prev]
+            act += ["L1_%d.%d" % (q, g) for q in c for g in range(2)] + ["L2_%d" % q for q in prev]
+        act += ["S2_%d" % q for q in CHUNKS[-1]] + ["L2_%d" % q for q in CHUNKS[-1]]
+        queues = {
+            "SP": [["LX0", "LW0", "LW1"] + ["LX%d" % q for q in (1, 2)] + ["LW5"] + ["LX%d" % q for q in range(3, NQ)] + ["ST%d" % q for q in quads]],
+            "ACT": [act],
+            "POOL": [["PA%d.%d" % (q, g) for q in quads for g in range(2)]],
+            "PE": [
+                ["A%d.%d" % (q, j) for q in quads for j in range(8)],
+                ["W4T%d" % k for k in range(4)],
+                ["O%d.%d" % (q, b) for q in quads for b in range(2)],
+                ["T%d.%d" % (q, b) for q in quads for b in range(2)],
+                ["W5T0", "W5T1"],
+                ["D%d.%d" % (q, k) for q in quads for k in range(8)],
+            ],
+            "DVE": [
+                ["B4", "W4Q0", "W4Q1"],
+                ["OE%d.%d" % (q, b) for q in quads for b in range(2)],
+                [n % (q, g) for q in quads for g in range(2) for n in ("MX%d.%d", "HQ%d.%d")],
+                [n for q in quads for n in ("XC%d" % q, "XE%d.0" % q, "XE%d.1" % q, "XS%d" % q, "XQ%d" % q)],
+                ["F2_%d" % q for q in quads],
+                ["W5E0", "W5E1", "W5Q"],
+                ["WG%d.%d" % (q, k) for q in quads for k in range(8)],
+            ],
+        }
+        plan(ops, queues, lambda name, slot: ops[name]["run"](slot))

@@ -19,9 +19,9 @@ NG = N_TOK // P
 NQ = 8
 CHUNKS = ((0, 1, 2), (3, 4, 5), (6, 7))
 DELTA = 2.0 ** -62
-BUFS = {"pt": 2, "pa": 2, "pd": 2, "po": 2, "xr": 1, "xg": 1, "S": 6, "Wg": 6, "Ag": 2, "Hc": 2, "w2": 3, "s2": 4}
+BUFS = {"pa": 3, "pv": 5, "xr": 1, "xg": 1, "S": 6, "Wg": 6, "Ag": 2, "Hc": 2, "w2": 3, "s2": 4}
 TABLE_LOAD = 1300
-HOP = 60
+HOP = 350
 
 
 def plan(ops, queues, emit):
@@ -105,7 +105,7 @@ def tile_implicitnet_pa_t_kernel(tc, h3, x_in, W4, b4, W5, b5, out):
             return [keep.tile(shape, dt, name="%s%d" % (name, i), align_bytes=64) for i in range(n)]
 
         bank = {}
-        for tag in ("pt", "pa", "pd", "po"):
+        for tag in ("pa", "pv"):
             bank[tag] = [psum.tile([P, 512], F32, name="%s%d" % (tag, i)) for i in range(BUFS[tag])]
 
         ident = sb([P, P], F32, "ident")
@@ -184,7 +184,7 @@ def tile_implicitnet_pa_t_kernel(tc, h3, x_in, W4, b4, W5, b5, out):
 
         def w4t(k):
             def run(sl):
-                pt = bank["pt"][sl["W4T%d" % k]]
+                pt = bank["pv"][sl["W4T%d" % k]]
                 for jj in range(2):
                     for u in range(2):
                         j = 2 * k + jj
@@ -193,7 +193,7 @@ def tile_implicitnet_pa_t_kernel(tc, h3, x_in, W4, b4, W5, b5, out):
 
         def w4e(k):
             def run(sl):
-                pt = bank["pt"][sl["W4T%d" % k]]
+                pt = bank["pv"][sl["W4T%d" % k]]
                 nc.scalar.copy(
                     out=words(w4g).rearrange("p (j m u) -> p j m u", j=8, u=2)[:, 2 * k : 2 * k + 2],
                     in_=pt[:].rearrange("p (j u m) -> p j m u", j=2, u=2),
@@ -206,14 +206,14 @@ def tile_implicitnet_pa_t_kernel(tc, h3, x_in, W4, b4, W5, b5, out):
             )
 
         for k in range(4):
-            op("W4T%d" % k, "PE", 260, ["LW%d" % (k // 2)], w4t(k), ring=("pt", ["W4E%d" % k]))
+            op("W4T%d" % k, "PE", 260, ["LW%d" % (k // 2)], w4t(k), ring=("pv", ["W4E%d" % k]))
             op("W4E%d" % k, "ACT", 450, ["W4T%d" % k], w4e(k))
         for h in range(2):
             op("W4Q%d" % h, "DVE", 470, ["W4E%d" % (2 * h), "W4E%d" % (2 * h + 1)], w4q(h))
 
         def w5t(g):
             def run(sl):
-                pt = bank["pt"][sl["W5T%d" % g]]
+                pt = bank["pv"][sl["W5T%d" % g]]
                 for a in range(2):
                     for u in range(2):
                         lo = 512 * a + 256 * g + u
@@ -222,7 +222,7 @@ def tile_implicitnet_pa_t_kernel(tc, h3, x_in, W4, b4, W5, b5, out):
 
         def w5e(g):
             def run(sl):
-                pt = bank["pt"][sl["W5T%d" % g]]
+                pt = bank["pv"][sl["W5T%d" % g]]
                 nc.vector.tensor_copy(
                     out=words(w5g).rearrange("p (g a n u) -> p g a n u", g=2, a=2, u=2)[:, g],
                     in_=pt[:].rearrange("p (a u n) -> p a n u", a=2, u=2),
@@ -230,7 +230,7 @@ def tile_implicitnet_pa_t_kernel(tc, h3, x_in, W4, b4, W5, b5, out):
             return run
 
         for g in range(2):
-            op("W5T%d" % g, "PE", 420, ["LW5"], w5t(g), ring=("pt", ["W5E%d" % g]))
+            op("W5T%d" % g, "PE", 420, ["LW5"], w5t(g), ring=("pv", ["W5E%d" % g]))
             op("W5E%d" % g, "DVE", 450, ["W5T%d" % g], w5e(g))
         op("W5Q", "DVE", 470, ["W5E0", "W5E1"], lambda sl: nc.vector.quantize_mx(out=w5c[:].bitcast(FP8X4), scales=w5s[:], in_=w5g[:]))
 
@@ -242,7 +242,7 @@ def tile_implicitnet_pa_t_kernel(tc, h3, x_in, W4, b4, W5, b5, out):
 
         def xt(q, b):
             def run(sl):
-                pt = bank["pt"][sl["T%d.%d" % (q, b)]]
+                pt = bank["pv"][sl["T%d.%d" % (q, b)]]
                 xw = X[q][:].rearrange("p g k -> p (g k)").bitcast(F32)
                 for ii in range(2):
                     for u in range(2):
@@ -252,7 +252,7 @@ def tile_implicitnet_pa_t_kernel(tc, h3, x_in, W4, b4, W5, b5, out):
 
         def xe(q, b):
             def run(sl):
-                pt = bank["pt"][sl["T%d.%d" % (q, b)]]
+                pt = bank["pv"][sl["T%d.%d" % (q, b)]]
                 nc.vector.tensor_copy(
                     out=words(xr[sl["XE%d.0" % q]]).rearrange("p (i r u) -> p i r u", i=4, u=2)[:, 2 * b : 2 * b + 2],
                     in_=pt[:].rearrange("p (i u r) -> p i r u", i=2, u=2),
@@ -277,7 +277,7 @@ def tile_implicitnet_pa_t_kernel(tc, h3, x_in, W4, b4, W5, b5, out):
 
         def l1d(q, k):
             def run(sl):
-                pd = bank["pd"][sl["D%d.%d" % (q, k)]]
+                pd = bank["pv"][sl["D%d.%d" % (q, k)]]
                 i, g = k // 2, k % 2
                 for t in range(4):
                     j = 4 * g + t
@@ -289,7 +289,7 @@ def tile_implicitnet_pa_t_kernel(tc, h3, x_in, W4, b4, W5, b5, out):
                 i, g = k // 2, k % 2
                 nc.vector.tensor_tensor(
                     out=Wg[sl["WG%d.%d" % (q, g)]][:].rearrange("p (i r t) -> p i r t", i=4, t=4)[:, i],
-                    in0=bank["pd"][sl["D%d.%d" % (q, k)]][:].rearrange("p (t r) -> p r t", t=4),
+                    in0=bank["pv"][sl["D%d.%d" % (q, k)]][:].rearrange("p (t r) -> p r t", t=4),
                     in1=b4f[:, 4 * g : 4 * g + 4].unsqueeze(1).to_broadcast([P, P, 4]),
                     op=ALU.add,
                 )
@@ -301,27 +301,24 @@ def tile_implicitnet_pa_t_kernel(tc, h3, x_in, W4, b4, W5, b5, out):
                 nc.scalar.activation(out=s, in_=s, func=FN.Ln, bias=dl[:], scale=1.0)
             return run
 
-        def pscale(q, g):
-            return lambda sl: nc.gpsimd.tensor_scalar(
-                out=Ag[sl["PA%d.%d" % (q, g)]][:].rearrange("p (x t) -> p x t", t=4),
-                in0=S[sl["S1_%d.%d" % (q, 4 * g)]][:].rearrange("p t x -> p x t"),
-                scalar1=-0.01, scalar2=0.0, op0=ALU.mult, op1=ALU.add,
-            )
-
         def hmax(q, g):
-            def run(sl):
-                a = Ag[sl["PA%d.%d" % (q, g)]]
-                nc.vector.tensor_tensor(out=a[:], in0=a[:], in1=Wg[sl["WG%d.%d" % (q, g)]][:], op=ALU.max)
-            return run
+            return lambda sl: nc.vector.scalar_tensor_tensor(
+                out=Ag[sl["MX%d.%d" % (q, g)]][:].rearrange("p (x t) -> p x t", t=4),
+                in0=S[sl["S1_%d.%d" % (q, 4 * g)]][:].rearrange("p t x -> p x t"),
+                scalar=-0.01,
+                in1=Wg[sl["WG%d.%d" % (q, g)]][:].rearrange("p (x t) -> p x t", t=4),
+                op0=ALU.mult,
+                op1=ALU.max,
+            )
 
         def hquant(q, g):
             return lambda sl: nc.vector.quantize_mx(
-                out=Hc[sl["HQ%d.0" % q]][:, g, :].bitcast(FP8X4), scales=Hs[sl["HQ%d.0" % q]][:, g, :], in_=Ag[sl["PA%d.%d" % (q, g)]][:]
+                out=Hc[sl["HQ%d.0" % q]][:, g, :].bitcast(FP8X4), scales=Hs[sl["HQ%d.0" % q]][:, g, :], in_=Ag[sl["MX%d.%d" % (q, g)]][:]
             )
 
         def l2(q, b):
             def run(sl):
-                po = bank["po"][sl["O%d.%d" % (q, b)]]
+                po = bank["pv"][sl["O%d.%d" % (q, b)]]
                 hc, hs = Hc[sl["HQ%d.0" % q]], Hs[sl["HQ%d.0" % q]]
                 for ii in range(2):
                     i = 2 * b + ii
@@ -332,7 +329,7 @@ def tile_implicitnet_pa_t_kernel(tc, h3, x_in, W4, b4, W5, b5, out):
         def oe(q, b):
             return lambda sl: nc.vector.tensor_tensor(
                 out=w2[sl["OE%d.0" % q]][:].rearrange("p (i n) -> p i n", i=4)[:, 2 * b : 2 * b + 2],
-                in0=bank["po"][sl["O%d.%d" % (q, b)]][:].rearrange("p (i n) -> p i n", i=2),
+                in0=bank["pv"][sl["O%d.%d" % (q, b)]][:].rearrange("p (i n) -> p i n", i=2),
                 in1=b5bc[:].unsqueeze(1).to_broadcast([P, 2, HC]),
                 op=ALU.add,
             )
@@ -354,23 +351,22 @@ def tile_implicitnet_pa_t_kernel(tc, h3, x_in, W4, b4, W5, b5, out):
         for q in range(NQ):
             op("XC%d" % q, "DVE", 150, ["LX%d" % q, 3500 + 500 * (q // 2)], xcat(q))
             for b in range(2):
-                op("T%d.%d" % (q, b), "PE", 260, ["XC%d" % q], xt(q, b), ring=("pt", ["XE%d.%d" % (q, b)]))
+                op("T%d.%d" % (q, b), "PE", 260, ["XC%d" % q], xt(q, b), ring=("pv", ["XE%d.%d" % (q, b)]))
                 op("XE%d.%d" % (q, b), "DVE", 450, ["T%d.%d" % (q, b)], xe(q, b), ring=("xr", ["XS%d" % q]) if b == 0 else None)
             op("XS%d" % q, "DVE", 450, ["XE%d.0" % q, "XE%d.1" % q], xscale(q), ring=("xg", ["XQ%d" % q]))
             op("XQ%d" % q, "DVE", 470, ["XS%d" % q], xquant(q))
             for j in range(8):
                 op("A%d.%d" % (q, j), "PE", 220, ["XQ%d" % q, "W4Q%d" % (j // 4)], l1a(q, j), ring=("pa", ["S1_%d.%d" % (q, j)]))
-                op("S1_%d.%d" % (q, j), "ACT", 472, ["A%d.%d" % (q, j), "B4"], sig1(q, j), ring=("S", ["PA%d.%d" % (q, j // 4)]) if j % 4 == 0 else None, fn="sig")
+                op("S1_%d.%d" % (q, j), "ACT", 472, ["A%d.%d" % (q, j), "B4"], sig1(q, j), ring=("S", ["MX%d.%d" % (q, j // 4)]) if j % 4 == 0 else None, fn="sig")
             for k in range(8):
-                op("D%d.%d" % (q, k), "PE", 246, ["XQ%d" % q, "W4Q%d" % (k % 2)], l1d(q, k), ring=("pd", ["WG%d.%d" % (q, k)]))
+                op("D%d.%d" % (q, k), "PE", 246, ["XQ%d" % q, "W4Q%d" % (k % 2)], l1d(q, k), ring=("pv", ["WG%d.%d" % (q, k)]))
                 op("WG%d.%d" % (q, k), "DVE", 480, ["D%d.%d" % (q, k), "B4"], wguard(q, k), ring=("Wg", ["MX%d.%d" % (q, k)]) if k < 2 else None)
             for g in range(2):
                 op("L1_%d.%d" % (q, g), "ACT", 1725, ["S1_%d.%d" % (q, 4 * g + t) for t in range(4)], ln1(q, g), fn="ln")
-                op("PA%d.%d" % (q, g), "POOL", 2150, ["L1_%d.%d" % (q, g)], pscale(q, g), ring=("Ag", ["HQ%d.%d" % (q, g)]))
-                op("MX%d.%d" % (q, g), "DVE", 870, ["PA%d.%d" % (q, g)] + ["WG%d.%d" % (q, 2 * i + g) for i in range(4)], hmax(q, g))
+                op("MX%d.%d" % (q, g), "DVE", 1760, ["L1_%d.%d" % (q, g)] + ["WG%d.%d" % (q, 2 * i + g) for i in range(4)], hmax(q, g), ring=("Ag", ["HQ%d.%d" % (q, g)]))
                 op("HQ%d.%d" % (q, g), "DVE", 470, ["MX%d.%d" % (q, g)], hquant(q, g), ring=("Hc", ["O%d.0" % q, "O%d.1" % q]) if g == 0 else None)
             for b in range(2):
-                op("O%d.%d" % (q, b), "PE", 444, ["HQ%d.0" % q, "HQ%d.1" % q, "W5Q"], l2(q, b), ring=("po", ["OE%d.%d" % (q, b)]))
+                op("O%d.%d" % (q, b), "PE", 444, ["HQ%d.0" % q, "HQ%d.1" % q, "W5Q"], l2(q, b), ring=("pv", ["OE%d.%d" % (q, b)]))
                 op("OE%d.%d" % (q, b), "DVE", 480, ["O%d.%d" % (q, b)], oe(q, b), ring=("w2", ["F2_%d" % q]) if b == 0 else None)
             op("S2_%d" % q, "ACT", 872, ["OE%d.0" % q, "OE%d.1" % q], sig2(q), ring=("s2", ["ST%d" % q]), fn="sig")
             op("L2_%d" % q, "ACT", 872, ["S2_%d" % q], ln2(q), fn="ln")
@@ -387,7 +383,6 @@ def tile_implicitnet_pa_t_kernel(tc, h3, x_in, W4, b4, W5, b5, out):
         queues = {
             "SP": [["LX0", "LW0", "LW1"] + ["LX%d" % q for q in (1, 2)] + ["LW5"] + ["LX%d" % q for q in range(3, NQ)] + ["ST%d" % q for q in quads]],
             "ACT": [act],
-            "POOL": [["PA%d.%d" % (q, g) for q in quads for g in range(2)]],
             "PE": [
                 ["A%d.%d" % (q, j) for q in quads for j in range(8)],
                 ["W4T%d" % k for k in range(4)],

@@ -19,7 +19,7 @@ NG = N_TOK // P
 NQ = 8
 CHUNKS = ((0, 1, 2), (3, 4, 5), (6, 7))
 DELTA = 2.0 ** -62
-BUFS = {"pa": 3, "pv": 5, "xr": 1, "xg": 1, "S": 6, "Wg": 6, "Ag": 2, "Hc": 2, "w2": 3, "s2": 4}
+BUFS = {"pa": 4, "pv": 4, "xr": 1, "xg": 1, "S": 6, "Wg": 6, "Ag": 2, "Hc": 2, "w2": 3, "s2": 4}
 TABLE_LOAD = 1300
 HOP = 350
 
@@ -142,10 +142,11 @@ def tile_implicitnet_pa_t_kernel(tc, h3, x_in, W4, b4, W5, b5, out):
         nc.scalar.activation(out=warm[:], in_=dl[:], func=FN.Sigmoid)
         make_identity(nc, ident[:])
         nc.scalar.dma_start(out=xin[:], in_=x_in.rearrange("(p g) c -> p (g c)", g=NG))
-        for a in range(4):
+        nc.scalar.dma_start(out=tail13[:, 0:8, 0:13], in_=h3v[:, 0:8, cut : HA - DIN])
+        nc.scalar.dma_start(out=b4b[:].rearrange("p (g t) -> p g t", g=2), in_=b4.rearrange("(g p t) -> p g t", g=2, t=4))
+        for a in range(1, 4):
             nc.scalar.dma_start(out=tail13[:, 8 * a : 8 * a + 8, 0:13], in_=h3v[:, 8 * a : 8 * a + 8, cut : HA - DIN])
-        nc.gpsimd.dma_start(out=b4b[:].rearrange("p (g t) -> p g t", g=2), in_=b4.rearrange("(g p t) -> p g t", g=2, t=4))
-        nc.gpsimd.dma_start(out=b5bc[:], in_=b5.partition_broadcast(P))
+        nc.scalar.dma_start(out=b5bc[:], in_=b5.partition_broadcast(P))
 
         ops = {}
 
@@ -180,7 +181,7 @@ def tile_implicitnet_pa_t_kernel(tc, h3, x_in, W4, b4, W5, b5, out):
             nc.vector.tensor_copy(out=b4f[:], in_=b4b[:])
             nc.vector.tensor_scalar(out=nb4[:], in0=b4b[:], scalar1=-100.0, scalar2=None, op0=ALU.mult)
 
-        op("B4", "DVE", 150, [3000], run_b4)
+        op("B4", "DVE", 150, [5500], run_b4)
 
         def w4t(k):
             def run(sl):
@@ -301,19 +302,22 @@ def tile_implicitnet_pa_t_kernel(tc, h3, x_in, W4, b4, W5, b5, out):
                 nc.scalar.activation(out=s, in_=s, func=FN.Ln, bias=dl[:], scale=1.0)
             return run
 
-        def hmax(q, g):
-            return lambda sl: nc.vector.scalar_tensor_tensor(
-                out=Ag[sl["MX%d.%d" % (q, g)]][:].rearrange("p (x t) -> p x t", t=4),
+        def pscale(q, g):
+            return lambda sl: nc.gpsimd.tensor_scalar(
+                out=Ag[sl["PA%d.%d" % (q, g)]][:].rearrange("p (x t) -> p x t", t=4),
                 in0=S[sl["S1_%d.%d" % (q, 4 * g)]][:].rearrange("p t x -> p x t"),
-                scalar=-0.01,
-                in1=Wg[sl["WG%d.%d" % (q, g)]][:].rearrange("p (x t) -> p x t", t=4),
-                op0=ALU.mult,
-                op1=ALU.max,
+                scalar1=-0.01, scalar2=0.0, op0=ALU.mult, op1=ALU.add,
             )
+
+        def hmax(q, g):
+            def run(sl):
+                a = Ag[sl["PA%d.%d" % (q, g)]]
+                nc.vector.tensor_tensor(out=a[:], in0=a[:], in1=Wg[sl["WG%d.%d" % (q, g)]][:], op=ALU.max)
+            return run
 
         def hquant(q, g):
             return lambda sl: nc.vector.quantize_mx(
-                out=Hc[sl["HQ%d.0" % q]][:, g, :].bitcast(FP8X4), scales=Hs[sl["HQ%d.0" % q]][:, g, :], in_=Ag[sl["MX%d.%d" % (q, g)]][:]
+                out=Hc[sl["HQ%d.0" % q]][:, g, :].bitcast(FP8X4), scales=Hs[sl["HQ%d.0" % q]][:, g, :], in_=Ag[sl["PA%d.%d" % (q, g)]][:]
             )
 
         def l2(q, b):
@@ -357,13 +361,14 @@ def tile_implicitnet_pa_t_kernel(tc, h3, x_in, W4, b4, W5, b5, out):
             op("XQ%d" % q, "DVE", 470, ["XS%d" % q], xquant(q))
             for j in range(8):
                 op("A%d.%d" % (q, j), "PE", 220, ["XQ%d" % q, "W4Q%d" % (j // 4)], l1a(q, j), ring=("pa", ["S1_%d.%d" % (q, j)]))
-                op("S1_%d.%d" % (q, j), "ACT", 472, ["A%d.%d" % (q, j), "B4"], sig1(q, j), ring=("S", ["MX%d.%d" % (q, j // 4)]) if j % 4 == 0 else None, fn="sig")
+                op("S1_%d.%d" % (q, j), "ACT", 472, ["A%d.%d" % (q, j), "B4"], sig1(q, j), ring=("S", ["PA%d.%d" % (q, j // 4)]) if j % 4 == 0 else None, fn="sig")
             for k in range(8):
                 op("D%d.%d" % (q, k), "PE", 246, ["XQ%d" % q, "W4Q%d" % (k % 2)], l1d(q, k), ring=("pv", ["WG%d.%d" % (q, k)]))
                 op("WG%d.%d" % (q, k), "DVE", 480, ["D%d.%d" % (q, k), "B4"], wguard(q, k), ring=("Wg", ["MX%d.%d" % (q, k)]) if k < 2 else None)
             for g in range(2):
                 op("L1_%d.%d" % (q, g), "ACT", 1725, ["S1_%d.%d" % (q, 4 * g + t) for t in range(4)], ln1(q, g), fn="ln")
-                op("MX%d.%d" % (q, g), "DVE", 1760, ["L1_%d.%d" % (q, g)] + ["WG%d.%d" % (q, 2 * i + g) for i in range(4)], hmax(q, g), ring=("Ag", ["HQ%d.%d" % (q, g)]))
+                op("PA%d.%d" % (q, g), "POOL", 2150, ["L1_%d.%d" % (q, g)], pscale(q, g), ring=("Ag", ["HQ%d.%d" % (q, g)]))
+                op("MX%d.%d" % (q, g), "DVE", 870, ["PA%d.%d" % (q, g)] + ["WG%d.%d" % (q, 2 * i + g) for i in range(4)], hmax(q, g))
                 op("HQ%d.%d" % (q, g), "DVE", 470, ["MX%d.%d" % (q, g)], hquant(q, g), ring=("Hc", ["O%d.0" % q, "O%d.1" % q]) if g == 0 else None)
             for b in range(2):
                 op("O%d.%d" % (q, b), "PE", 444, ["HQ%d.0" % q, "HQ%d.1" % q, "W5Q"], l2(q, b), ring=("pv", ["OE%d.%d" % (q, b)]))
@@ -383,6 +388,7 @@ def tile_implicitnet_pa_t_kernel(tc, h3, x_in, W4, b4, W5, b5, out):
         queues = {
             "SP": [["LX0", "LW0", "LW1"] + ["LX%d" % q for q in (1, 2)] + ["LW5"] + ["LX%d" % q for q in range(3, NQ)] + ["ST%d" % q for q in quads]],
             "ACT": [act],
+            "POOL": [["PA%d.%d" % (q, g) for q in quads for g in range(2)]],
             "PE": [
                 ["A%d.%d" % (q, j) for q in quads for j in range(8)],
                 ["W4T%d" % k for k in range(4)],

@@ -17,11 +17,11 @@ N_TOK, HA, HB, HC, DIN = 4096, 512, 1024, 256, 3
 FLOPS = 2 * N_TOK * HA * HB + 2 * N_TOK * HB * HC
 NG = N_TOK // P
 NQ = 8
-CHUNKS = ((0, 1, 2), (3, 4, 5), (6, 7))
+CHUNKS = ((0, 1), (2, 3, 4), (5, 6), (7,))
 DELTA = 2.0 ** -62
-BUFS = {"pa": 4, "pv": 4, "xr": 1, "xg": 1, "S": 6, "Wg": 6, "Ag": 2, "Hc": 2, "w2": 3, "s2": 4}
+BUFS = {"pa": 4, "pv": 4, "xr": 1, "xg": 1, "S": 6, "Wg": 6, "Ag": 2, "Hc": 2, "w2": 4, "s2": 4}
 TABLE_LOAD = 1300
-HOP = 350
+HOP = 550
 
 
 def plan(ops, queues, emit):
@@ -30,7 +30,7 @@ def plan(ops, queues, emit):
     ptr = {}
     uses = {}
     slot = {}
-    state = {"fn": None}
+    state = {"fn": None, "port": 0}
     for e in queues:
         free[e] = 0
         ptr[e] = [0 for c in queues[e]]
@@ -53,6 +53,8 @@ def plan(ops, queues, emit):
                 return None
             else:
                 t = max(t, end[d] + (0 if ops[d]["eng"] == e else HOP))
+        if op["port"]:
+            t = max(t, state["port"])
         return t
 
     done = 0
@@ -83,6 +85,8 @@ def plan(ops, queues, emit):
             uses[tag] = used + [op["ring"][1]]
         end[name] = t + op["cost"]
         free[e] = end[name]
+        if op["port"]:
+            state["port"] = end[name]
         ptr[e][ci] += 1
         done += 1
         emit(name, slot)
@@ -151,7 +155,8 @@ def tile_implicitnet_pa_t_kernel(tc, h3, x_in, W4, b4, W5, b5, out):
         ops = {}
 
         def op(name, eng, cost, deps, run, ring=None, fn=None):
-            ops[name] = {"eng": eng, "cost": cost, "deps": deps, "ring": ring, "fn": fn, "run": run}
+            port = eng == "POOL" or (eng == "DVE" and name[:2] in ("XS", "XQ", "MX", "HQ", "F2", "W4", "W5", "XC"))
+            ops[name] = {"eng": eng, "cost": cost, "deps": deps, "ring": ring, "fn": fn, "run": run, "port": port}
 
         def words(t):
             return t[:].bitcast(F32)
@@ -380,13 +385,17 @@ def tile_implicitnet_pa_t_kernel(tc, h3, x_in, W4, b4, W5, b5, out):
 
         quads = [q for c in CHUNKS for q in c]
         act = ["W4E%d" % k for k in range(4)]
-        for ci, c in enumerate(CHUNKS):
-            prev = CHUNKS[ci - 1] if ci > 0 else ()
-            act += ["S1_%d.%d" % (q, j) for q in c for j in range(8)] + ["S2_%d" % q for q in prev]
-            act += ["L1_%d.%d" % (q, g) for q in c for g in range(2)] + ["L2_%d" % q for q in prev]
-        act += ["S2_%d" % q for q in CHUNKS[-1]] + ["L2_%d" % q for q in CHUNKS[-1]]
+        second = []
+        pending = []
+        for c in CHUNKS:
+            now, pending = pending[:-1], pending[-1:] + list(c)
+            second += now
+            act += ["S1_%d.%d" % (q, j) for q in c for j in range(8)] + ["S2_%d" % q for q in now]
+            act += ["L1_%d.%d" % (q, g) for q in c for g in range(2)] + ["L2_%d" % q for q in now]
+        second += pending
+        act += ["S2_%d" % q for q in pending] + ["L2_%d" % q for q in pending]
         queues = {
-            "SP": [["LX0", "LW0", "LW1"] + ["LX%d" % q for q in (1, 2)] + ["LW5"] + ["LX%d" % q for q in range(3, NQ)] + ["ST%d" % q for q in quads]],
+            "SP": [["LX0", "LW0", "LW1"] + ["LX%d" % q for q in (1, 2)] + ["LW5"] + ["LX%d" % q for q in range(3, NQ)] + ["ST%d" % q for q in second]],
             "ACT": [act],
             "POOL": [["PA%d.%d" % (q, g) for q in quads for g in range(2)]],
             "PE": [
@@ -399,10 +408,10 @@ def tile_implicitnet_pa_t_kernel(tc, h3, x_in, W4, b4, W5, b5, out):
             ],
             "DVE": [
                 ["B4", "W4Q0", "W4Q1"],
-                ["OE%d.%d" % (q, b) for q in quads for b in range(2)],
                 [n % (q, g) for q in quads for g in range(2) for n in ("MX%d.%d", "HQ%d.%d")],
+                ["OE%d.%d" % (q, b) for q in quads for b in range(2)],
                 [n for q in quads for n in ("XC%d" % q, "XE%d.0" % q, "XE%d.1" % q, "XS%d" % q, "XQ%d" % q)],
-                ["F2_%d" % q for q in quads],
+                ["F2_%d" % q for q in second],
                 ["W5E0", "W5E1", "W5Q"],
                 ["WG%d.%d" % (q, k) for q in quads for k in range(8)],
             ],

@@ -11,152 +11,86 @@ U8 = mybir.dt.uint8
 FP8X4 = mybir.dt.float8_e4m3fn_x4
 ALU = mybir.AluOpType
 FN = mybir.ActivationFunctionType
+ENG = mybir.EngineType
 
 P = 128
 N_TOK, HA, HB, HC, DIN = 4096, 512, 1024, 256, 3
 FLOPS = 2 * N_TOK * HA * HB + 2 * N_TOK * HB * HC
 NG = N_TOK // P
 NQ = 8
-CHUNKS = ((0, 1), (2, 3, 4), (5, 6), (7,))
+CUT = 496
 DELTA = 2.0 ** -62
-BUFS = {"pa": 4, "pv": 4, "xr": 1, "xg": 1, "S": 6, "Wg": 6, "Ag": 2, "Hc": 2, "w2": 4, "s2": 4}
-TABLE_LOAD = 1300
-HOP = 550
+CHUNKS = (4, 6, 4, 2)
+SECOND = ((), (), (), (0, 1, 2), (3, 4, 5, 6, 7))
 
 
-def plan(ops, queues, emit):
-    end = {}
-    free = {}
-    ptr = {}
-    uses = {}
-    slot = {}
-    state = {"fn": None, "port": 0}
-    for e in queues:
-        free[e] = 0
-        ptr[e] = [0 for c in queues[e]]
-    total = sum(len(c) for e in queues for c in queues[e])
-    assert total == len(ops), (total, len(ops))
-
-    def ready(e, name):
-        op = ops[name]
-        t = free[e]
-        deps = list(op["deps"])
-        if op["ring"] is not None:
-            tag = op["ring"][0]
-            used = uses.get(tag, [])
-            if len(used) >= BUFS[tag]:
-                deps.extend(used[len(used) - BUFS[tag]])
-        for d in deps:
-            if isinstance(d, int):
-                t = max(t, d)
-            elif d not in end:
-                return None
-            else:
-                t = max(t, end[d] + (0 if ops[d]["eng"] == e else HOP))
-        if op["port"]:
-            t = max(t, state["port"])
-        return t
-
-    done = 0
-    while done < total:
-        best = None
-        for e in queues:
-            for ci, c in enumerate(queues[e]):
-                if ptr[e][ci] >= len(c):
-                    continue
-                t = ready(e, c[ptr[e][ci]])
-                if t is None:
-                    continue
-                key = (t, ci)
-                if best is None or key < best[0]:
-                    best = (key, e, ci)
-        assert best is not None, "the plan is stuck"
-        key, e, ci = best
-        name = queues[e][ci][ptr[e][ci]]
-        op = ops[name]
-        t = key[0]
-        if op["fn"] is not None and op["fn"] != state["fn"]:
-            t = max(t, free[e] + TABLE_LOAD)
-            state["fn"] = op["fn"]
-        if op["ring"] is not None:
-            tag = op["ring"][0]
-            used = uses.get(tag, [])
-            slot[name] = len(used) % BUFS[tag]
-            uses[tag] = used + [op["ring"][1]]
-        end[name] = t + op["cost"]
-        free[e] = end[name]
-        if op["port"]:
-            state["port"] = end[name]
-        ptr[e][ci] += 1
-        done += 1
-        emit(name, slot)
+def weave(queues):
+    done = set()
+    heads = [0 for q in queues]
+    left = sum(len(q) for q in queues)
+    while left:
+        before = left
+        for i, q in enumerate(queues):
+            if heads[i] < len(q):
+                name, needs, run = q[heads[i]]
+                if all(n in done for n in needs):
+                    run()
+                    done.add(name)
+                    heads[i] += 1
+                    left -= 1
+        assert left < before, "the queues wait for each other"
 
 
 def tile_implicitnet_pa_t_kernel(tc, h3, x_in, W4, b4, W5, b5, out):
     nc = tc.nc
     h3v = h3.rearrange("(p g) k -> p g k", g=NG)
     outv = out.rearrange("(p g) n -> p g n", g=NG)
-    cut = 496
 
     with ExitStack() as ctx:
-        keep = ctx.enter_context(tc.tile_pool(name="keep", bufs=1))
+        pool = ctx.enter_context(tc.tile_pool(name="sb", bufs=1))
         psum = ctx.enter_context(tc.psum_pool(name="psum", bufs=1))
-        ctx.enter_context(tc.manual_schedule())
+        ctx.enter_context(tc.manual_schedule(engines={ENG.Activation, ENG.DVE, ENG.Pool, ENG.SP}))
 
-        def sb(shape, dt, name, n=None):
-            if n is None:
-                return keep.tile(shape, dt, name=name, align_bytes=64)
-            return [keep.tile(shape, dt, name="%s%d" % (name, i), align_bytes=64) for i in range(n)]
+        def keep(shape, dt, name):
+            return pool.tile(shape, dt, name=name, align_bytes=64)
 
-        bank = {}
-        for tag in ("pa", "pv"):
-            bank[tag] = [psum.tile([P, 512], F32, name="%s%d" % (tag, i)) for i in range(BUFS[tag])]
+        def ring(shape, dt, tag, bufs):
+            return pool.tile(shape, dt, name=tag, tag=tag, bufs=bufs, align_bytes=64)
 
-        ident = sb([P, P], F32, "ident")
-        dl = sb([P, 1], F32, "dl")
-        warm = sb([P, 1], F32, "warm")
-        b4b = sb([P, 8], BF16, "b4b")
-        b4f = sb([P, 8], F32, "b4f")
-        nb4 = sb([P, 8], F32, "nb4")
-        b5bc = sb([P, HC], BF16, "b5bc")
-        tail13 = sb([P, NG, 16], BF16, "tail13")
-        xin = sb([P, NG * DIN], BF16, "xin")
-        X = sb([P, 4, HA], BF16, "X", NQ)
-        xr = sb([P, 2048], BF16, "xr", BUFS["xr"])
-        xg = sb([P, 2048], BF16, "xg", BUFS["xg"])
-        xc = sb([P, 512], U32, "xc", NQ)
-        xs = sb([P, 512], U8, "xs", NQ)
-        w4sb = sb([P, 8 * HA], BF16, "w4sb")
-        w4g = sb([P, 8 * HA], BF16, "w4g")
-        w4c = sb([P, HB], U32, "w4c")
-        w4s = sb([P, HB], U8, "w4s")
-        w5sb = sb([P, 2 * HB], BF16, "w5sb")
-        w5g = sb([P, 2 * HB], BF16, "w5g")
-        w5c = sb([P, 512], U32, "w5c")
-        w5s = sb([P, 512], U8, "w5s")
-        S = sb([P, 4, 512], F32, "S", BUFS["S"])
-        Wg = sb([P, 2048], BF16, "Wg", BUFS["Wg"])
-        Ag = sb([P, 2048], BF16, "Ag", BUFS["Ag"])
-        Hc = sb([P, 2, 512], U32, "Hc", BUFS["Hc"])
-        Hs = sb([P, 2, 512], U8, "Hs", BUFS["Hc"])
-        w2 = sb([P, 1024], F32, "w2", BUFS["w2"])
-        s2 = sb([P, 1024], F32, "s2", BUFS["s2"])
+        def bank(tag, bufs):
+            return psum.tile([P, 512], F32, name=tag, tag=tag, bufs=bufs)
+
+        def big(shape, dt):
+            return ring(shape, dt, "S", 13)
+
+        ident = keep([P, P], F32, "ident")
+        dl = keep([P, 1], F32, "dl")
+        warm = keep([P, 1], F32, "warm")
+        b4b = keep([P, 8], BF16, "b4b")
+        b4f = keep([P, 8], F32, "b4f")
+        pb4 = keep([P, 8], F32, "pb4")
+        b5bc = keep([P, HC], BF16, "b5bc")
+        tail13 = keep([P, NG, 16], BF16, "tail13")
+        xin = keep([P, NG * DIN], BF16, "xin")
+        X = [keep([P, 4, HA], BF16, "X%d" % q) for q in range(NQ)]
+        xc = [keep([P, 512], U32, "xc%d" % q) for q in range(NQ)]
+        xs = [keep([P, 512], U8, "xs%d" % q) for q in range(NQ)]
+        w4c = keep([P, HB], U32, "w4c")
+        w4s = keep([P, HB], U8, "w4s")
+        w5c = keep([P, 512], U32, "w5c")
+        w5s = keep([P, 512], U8, "w5s")
 
         nc.vector.memset(dl[:], DELTA)
-        nc.scalar.activation(out=warm[:], in_=dl[:], func=FN.Sigmoid)
         make_identity(nc, ident[:])
         nc.scalar.dma_start(out=xin[:], in_=x_in.rearrange("(p g) c -> p (g c)", g=NG))
-        nc.scalar.dma_start(out=tail13[:, 0:8, 0:13], in_=h3v[:, 0:8, cut : HA - DIN])
+        nc.scalar.dma_start(out=tail13[:, 0:8, 0:13], in_=h3v[:, 0:8, CUT : HA - DIN])
         nc.scalar.dma_start(out=b4b[:].rearrange("p (g t) -> p g t", g=2), in_=b4.rearrange("(g p t) -> p g t", g=2, t=4))
+        nc.scalar.activation(out=warm[:], in_=dl[:], func=FN.Sigmoid)
         for a in range(1, 4):
-            nc.scalar.dma_start(out=tail13[:, 8 * a : 8 * a + 8, 0:13], in_=h3v[:, 8 * a : 8 * a + 8, cut : HA - DIN])
+            nc.scalar.dma_start(out=tail13[:, 8 * a : 8 * a + 8, 0:13], in_=h3v[:, 8 * a : 8 * a + 8, CUT : HA - DIN])
         nc.scalar.dma_start(out=b5bc[:], in_=b5.partition_broadcast(P))
 
-        ops = {}
-
-        def op(name, eng, cost, deps, run, ring=None, fn=None):
-            port = eng == "POOL" or (eng == "DVE" and name[:2] in ("XS", "XQ", "MX", "HQ", "F2", "W4", "W5", "XC"))
-            ops[name] = {"eng": eng, "cost": cost, "deps": deps, "ring": ring, "fn": fn, "run": run, "port": port}
+        tiles = {}
 
         def words(t):
             return t[:].bitcast(F32)
@@ -164,256 +98,255 @@ def tile_implicitnet_pa_t_kernel(tc, h3, x_in, W4, b4, W5, b5, out):
         def mx(o, lw, ls, rw, rs, start, stop):
             nc.tensor.matmul_mx(out=o, lhsT=lw.bitcast(FP8X4), lhsT_scale=ls, rhs=rw.bitcast(FP8X4), rhs_scale=rs, start=start, stop=stop)
 
+        sp, act, gp, dve = [], [], [], []
+        pe_t, pe_a, pe_d, pe_o = [], [], [], []
+
+        def add(queue, name, needs, run, *args):
+            queue.append((name, needs, lambda: run(*args)))
+
         def ld_x(q):
-            return lambda sl: nc.sync.dma_start(out=X[q][:, :, 0:cut], in_=h3v[:, 4 * q : 4 * q + 4, 0:cut])
+            nc.sync.dma_start(out=X[q][:, :, 0:CUT], in_=h3v[:, 4 * q : 4 * q + 4, 0:CUT])
 
         def ld_w4(h):
-            return lambda sl: nc.sync.dma_start(
-                out=w4sb[:, 2048 * h : 2048 * h + 2048], in_=W4.rearrange("(g m t) k -> m g (t k)", g=2, t=4)[:, h, :]
-            )
+            if h == 0:
+                tiles["w4"] = big([P, 8 * HA], BF16)
+            nc.sync.dma_start(out=tiles["w4"][:, 2048 * h : 2048 * h + 2048], in_=W4.rearrange("(g m t) k -> m g (t k)", g=2, t=4)[:, h, :])
 
-        def ld_w5(sl):
-            nc.sync.dma_start(out=w5sb[:].rearrange("p (a k) -> p a k", a=2), in_=W5.rearrange("(a n) k -> n a k", a=2))
+        def ld_w5():
+            tiles["w5"] = big([P, 2 * HB], BF16)
+            nc.sync.dma_start(out=tiles["w5"][:].rearrange("p (a k) -> p a k", a=2), in_=W5.rearrange("(a n) k -> n a k", a=2))
 
-        op("LX0", "SP", 3000, [], ld_x(0))
-        op("LW0", "SP", 1000, [], ld_w4(0))
-        op("LW1", "SP", 1000, [], ld_w4(1))
-        for q in range(1, NQ):
-            op("LX%d" % q, "SP", 1000, [], ld_x(q))
-        op("LW5", "SP", 1000, [], ld_w5)
+        add(sp, "LX0", [], ld_x, 0)
+        add(sp, "LW0", [], ld_w4, 0)
+        add(sp, "LW1", [], ld_w4, 1)
+        add(sp, "LX1", [], ld_x, 1)
+        add(sp, "LX2", [], ld_x, 2)
+        add(sp, "LW5", [], ld_w5)
+        for q in range(3, NQ):
+            add(sp, "LX%d" % q, [], ld_x, q)
 
-        def run_b4(sl):
+        def run_b4():
             nc.vector.tensor_copy(out=b4f[:], in_=b4b[:])
-            nc.vector.tensor_scalar(out=nb4[:], in0=b4b[:], scalar1=-100.0, scalar2=None, op0=ALU.mult)
-
-        op("B4", "DVE", 150, [5500], run_b4)
+            nc.vector.tensor_scalar(out=pb4[:], in0=b4b[:], scalar1=100.0, scalar2=None, op0=ALU.mult)
 
         def w4t(k):
-            def run(sl):
-                pt = bank["pv"][sl["W4T%d" % k]]
-                for jj in range(2):
-                    for u in range(2):
-                        j = 2 * k + jj
-                        nc.tensor.transpose(pt[:, 256 * jj + 128 * u : 256 * jj + 128 * u + 128], words(w4sb)[:, 256 * j + 128 * u : 256 * j + 128 * u + 128], ident[:])
-            return run
+            tiles["w4t", k] = pt = bank("pd", 2)
+            for jj in range(2):
+                for u in range(2):
+                    j = 2 * k + jj
+                    nc.tensor.transpose(pt[:, 256 * jj + 128 * u : 256 * jj + 128 * u + 128], words(tiles["w4"])[:, 256 * j + 128 * u : 256 * j + 128 * u + 128], ident[:])
 
         def w4e(k):
-            def run(sl):
-                pt = bank["pv"][sl["W4T%d" % k]]
-                nc.scalar.copy(
-                    out=words(w4g).rearrange("p (j m u) -> p j m u", j=8, u=2)[:, 2 * k : 2 * k + 2],
-                    in_=pt[:].rearrange("p (j u m) -> p j m u", j=2, u=2),
-                )
-            return run
+            if k == 0:
+                tiles["w4g"] = big([P, 8 * HA], BF16)
+            nc.scalar.copy(
+                out=words(tiles["w4g"]).rearrange("p (j m u) -> p j m u", j=8, u=2)[:, 2 * k : 2 * k + 2],
+                in_=tiles["w4t", k][:].rearrange("p (j u m) -> p j m u", j=2, u=2),
+            )
 
         def w4q(h):
-            return lambda sl: nc.vector.quantize_mx(
-                out=w4c[:, 512 * h : 512 * h + 512].bitcast(FP8X4), scales=w4s[:, 512 * h : 512 * h + 512], in_=w4g[:, 2048 * h : 2048 * h + 2048]
-            )
-
-        for k in range(4):
-            op("W4T%d" % k, "PE", 260, ["LW%d" % (k // 2)], w4t(k), ring=("pv", ["W4E%d" % k]))
-            op("W4E%d" % k, "ACT", 450, ["W4T%d" % k], w4e(k))
-        for h in range(2):
-            op("W4Q%d" % h, "DVE", 470, ["W4E%d" % (2 * h), "W4E%d" % (2 * h + 1)], w4q(h))
+            nc.vector.quantize_mx(out=w4c[:, 512 * h : 512 * h + 512].bitcast(FP8X4), scales=w4s[:, 512 * h : 512 * h + 512], in_=tiles["w4g"][:, 2048 * h : 2048 * h + 2048])
 
         def w5t(g):
-            def run(sl):
-                pt = bank["pv"][sl["W5T%d" % g]]
-                for a in range(2):
-                    for u in range(2):
-                        lo = 512 * a + 256 * g + u
-                        nc.tensor.transpose(pt[:, 256 * a + 128 * u : 256 * a + 128 * u + 128], words(w5sb)[:, lo : lo + 255 : 2], ident[:])
-            return run
+            tiles["w5t", g] = pt = bank("px", 3)
+            for a in range(2):
+                for u in range(2):
+                    lo = 512 * a + 256 * g + u
+                    nc.tensor.transpose(pt[:, 256 * a + 128 * u : 256 * a + 128 * u + 128], words(tiles["w5"])[:, lo : lo + 255 : 2], ident[:])
 
         def w5e(g):
-            def run(sl):
-                pt = bank["pv"][sl["W5T%d" % g]]
-                nc.vector.tensor_copy(
-                    out=words(w5g).rearrange("p (g a n u) -> p g a n u", g=2, a=2, u=2)[:, g],
-                    in_=pt[:].rearrange("p (a u n) -> p a n u", a=2, u=2),
-                )
-            return run
+            if g == 0:
+                tiles["w5g"] = big([P, 2 * HB], BF16)
+            nc.vector.tensor_copy(
+                out=words(tiles["w5g"]).rearrange("p (g a n u) -> p g a n u", g=2, a=2, u=2)[:, g],
+                in_=tiles["w5t", g][:].rearrange("p (a u n) -> p a n u", a=2, u=2),
+            )
 
-        for g in range(2):
-            op("W5T%d" % g, "PE", 420, ["LW5"], w5t(g), ring=("pv", ["W5E%d" % g]))
-            op("W5E%d" % g, "DVE", 450, ["W5T%d" % g], w5e(g))
-        op("W5Q", "DVE", 470, ["W5E0", "W5E1"], lambda sl: nc.vector.quantize_mx(out=w5c[:].bitcast(FP8X4), scales=w5s[:], in_=w5g[:]))
+        def w5q():
+            nc.vector.quantize_mx(out=w5c[:].bitcast(FP8X4), scales=w5s[:], in_=tiles["w5g"][:])
 
         def xcat(q):
-            def run(sl):
-                nc.vector.tensor_copy(out=X[q][:, :, cut : HA - DIN], in_=tail13[:, 4 * q : 4 * q + 4, 0:13])
-                nc.vector.tensor_copy(out=X[q][:, :, HA - DIN : HA], in_=xin[:].rearrange("p (g c) -> p g c", c=DIN)[:, 4 * q : 4 * q + 4, :])
-            return run
+            nc.gpsimd.tensor_copy(out=X[q][:, :, CUT : HA - DIN], in_=tail13[:, 4 * q : 4 * q + 4, 0:13])
+            nc.gpsimd.tensor_copy(out=X[q][:, :, HA - DIN : HA], in_=xin[:].rearrange("p (g c) -> p g c", c=DIN)[:, 4 * q : 4 * q + 4, :])
 
         def xt(q, b):
-            def run(sl):
-                pt = bank["pv"][sl["T%d.%d" % (q, b)]]
-                xw = X[q][:].rearrange("p g k -> p (g k)").bitcast(F32)
-                for ii in range(2):
-                    for u in range(2):
-                        lo = 256 * (2 * b + ii) + 128 * u
-                        nc.tensor.transpose(pt[:, 256 * ii + 128 * u : 256 * ii + 128 * u + 128], xw[:, lo : lo + 128], ident[:])
-            return run
+            tiles["xt", q, b] = pt = bank("px", 3)
+            xw = X[q][:].rearrange("p g k -> p (g k)").bitcast(F32)
+            for ii in range(2):
+                for u in range(2):
+                    lo = 256 * (2 * b + ii) + 128 * u
+                    nc.tensor.transpose(pt[:, 256 * u + 128 * ii : 256 * u + 128 * ii + 128], xw[:, lo : lo + 128], ident[:])
 
         def xe(q, b):
-            def run(sl):
-                pt = bank["pv"][sl["T%d.%d" % (q, b)]]
-                nc.vector.tensor_copy(
-                    out=words(xr[sl["XE%d.0" % q]]).rearrange("p (i r u) -> p i r u", i=4, u=2)[:, 2 * b : 2 * b + 2],
-                    in_=pt[:].rearrange("p (i u r) -> p i r u", i=2, u=2),
-                )
-            return run
-
-        def xscale(q):
-            return lambda sl: nc.vector.tensor_scalar(
-                out=xg[sl["XS%d" % q]][:], in0=xr[sl["XE%d.0" % q]][:], scalar1=math.sqrt(0.5), scalar2=None, op0=ALU.mult
+            if b == 0:
+                tiles["xg", q] = ring([P, 2048], BF16, "xg", 2)
+            nc.vector.tensor_scalar(
+                out=tiles["xg", q][:, 1024 * b : 1024 * b + 1024].rearrange("p (x u e) -> p x u e", u=2, e=2),
+                in0=tiles["xt", q, b][:].bitcast(BF16).rearrange("p (u x e) -> p x u e", u=2, e=2),
+                scalar1=math.sqrt(0.5), scalar2=None, op0=ALU.mult,
             )
 
-        def xquant(q):
-            return lambda sl: nc.vector.quantize_mx(out=xc[q][:].bitcast(FP8X4), scales=xs[q][:], in_=xg[sl["XS%d" % q]][:])
+        def xq(q):
+            nc.vector.quantize_mx(out=xc[q][:].bitcast(FP8X4), scales=xs[q][:], in_=tiles["xg", q][:])
 
-        def l1a(q, j):
-            return lambda sl: mx(bank["pa"][sl["A%d.%d" % (q, j)]][:], w4c[:, 128 * j : 128 * j + 128], w4s[:, 128 * j : 128 * j + 128], xc[q][:], xs[q][:], True, True)
+        def l1a(n, t):
+            q, j = n // 2, 4 * (n % 2) + t
+            tiles["a", n, t] = pa = bank("pa", 3)
+            mx(pa[:], w4c[:, 128 * j : 128 * j + 128], w4s[:, 128 * j : 128 * j + 128], xc[q][:], xs[q][:], True, True)
 
-        def sig1(q, j):
-            return lambda sl: nc.scalar.activation(
-                out=S[sl["S1_%d.%d" % (q, 4 * (j // 4))]][:, j % 4, :], in_=bank["pa"][sl["A%d.%d" % (q, j)]][:], func=FN.Sigmoid, bias=nb4[:, j : j + 1], scale=-100.0
+        def sig1(n, t):
+            j = 4 * (n % 2) + t
+            if t == 0:
+                tiles["S", n] = big([P, 4, 512], F32)
+            nc.scalar.activation(out=tiles["S", n][:, t, :], in_=tiles["a", n, t][:], func=FN.Sigmoid, bias=pb4[:, j : j + 1], scale=100.0)
+
+        def ln1(n):
+            s = tiles["S", n][:].rearrange("p t x -> p (t x)")
+            nc.scalar.activation(out=s, in_=s, func=FN.Ln, bias=dl[:], scale=1.0)
+
+        def base(n, t):
+            j = 4 * (n % 2) + t
+            s = tiles["S", n][:, t, :]
+            nc.gpsimd.tensor_scalar(out=s, in0=s, scalar1=-0.01, scalar2=b4f[:, j : j + 1], op0=ALU.mult, op1=ALU.add)
+
+        def l1d(n, i):
+            q, g = n // 2, n % 2
+            tiles["d", n, i] = pd = bank("pd", 2)
+            for t in range(4):
+                j = 4 * g + t
+                mx(pd[:, 128 * t : 128 * t + 128], w4c[:, 128 * j : 128 * j + 128], w4s[:, 128 * j : 128 * j + 128], xc[q][:, 128 * i : 128 * i + 128], xs[q][:, 128 * i : 128 * i + 128], True, True)
+
+        def hsum(n, i):
+            if i == 0:
+                tiles["H", n] = ring([P, 2048], BF16, "H", 2)
+            nc.vector.tensor_tensor(
+                out=tiles["H", n][:].rearrange("p (i r t) -> p i r t", i=4, t=4)[:, i],
+                in0=tiles["d", n, i][:].rearrange("p (t r) -> p r t", t=4),
+                in1=tiles["S", n][:].rearrange("p t (i r) -> p i r t", i=4)[:, i],
+                op=ALU.add,
             )
 
-        def l1d(q, k):
-            def run(sl):
-                pd = bank["pv"][sl["D%d.%d" % (q, k)]]
-                i, g = k // 2, k % 2
-                for t in range(4):
-                    j = 4 * g + t
-                    mx(pd[:, 128 * t : 128 * t + 128], w4c[:, 128 * j : 128 * j + 128], w4s[:, 128 * j : 128 * j + 128], xc[q][:, 128 * i : 128 * i + 128], xs[q][:, 128 * i : 128 * i + 128], True, True)
-            return run
+        def hrelu(n):
+            h = tiles["H", n]
+            nc.vector.tensor_scalar(out=h[:], in0=h[:], scalar1=0.0, scalar2=None, op0=ALU.max)
 
-        def wguard(q, k):
-            def run(sl):
-                i, g = k // 2, k % 2
-                nc.vector.tensor_tensor(
-                    out=Wg[sl["WG%d.%d" % (q, g)]][:].rearrange("p (i r t) -> p i r t", i=4, t=4)[:, i],
-                    in0=bank["pv"][sl["D%d.%d" % (q, k)]][:].rearrange("p (t r) -> p r t", t=4),
-                    in1=b4f[:, 4 * g : 4 * g + 4].unsqueeze(1).to_broadcast([P, P, 4]),
-                    op=ALU.add,
-                )
-            return run
-
-        def ln1(q, g):
-            def run(sl):
-                s = S[sl["S1_%d.%d" % (q, 4 * g)]][:].rearrange("p t x -> p (t x)")
-                nc.scalar.activation(out=s, in_=s, func=FN.Ln, bias=dl[:], scale=1.0)
-            return run
-
-        def pscale(q, g):
-            return lambda sl: nc.gpsimd.tensor_scalar(
-                out=Ag[sl["PA%d.%d" % (q, g)]][:].rearrange("p (x t) -> p x t", t=4),
-                in0=S[sl["S1_%d.%d" % (q, 4 * g)]][:].rearrange("p t x -> p x t"),
-                scalar1=-0.01, scalar2=0.0, op0=ALU.mult, op1=ALU.add,
-            )
-
-        def hmax(q, g):
-            def run(sl):
-                a = Ag[sl["PA%d.%d" % (q, g)]]
-                nc.vector.tensor_tensor(out=a[:], in0=a[:], in1=Wg[sl["WG%d.%d" % (q, g)]][:], op=ALU.max)
-            return run
-
-        def hquant(q, g):
-            return lambda sl: nc.vector.quantize_mx(
-                out=Hc[sl["HQ%d.0" % q]][:, g, :].bitcast(FP8X4), scales=Hs[sl["HQ%d.0" % q]][:, g, :], in_=Ag[sl["PA%d.%d" % (q, g)]][:]
-            )
+        def hquant(n):
+            q, g = n // 2, n % 2
+            if g == 0:
+                tiles["Hc", q] = ring([P, 2, 512], U32, "Hc", 2)
+                tiles["Hs", q] = ring([P, 2, 512], U8, "Hs", 2)
+            nc.vector.quantize_mx(out=tiles["Hc", q][:, g, :].bitcast(FP8X4), scales=tiles["Hs", q][:, g, :], in_=tiles["H", n][:])
 
         def l2(q, b):
-            def run(sl):
-                po = bank["pv"][sl["O%d.%d" % (q, b)]]
-                hc, hs = Hc[sl["HQ%d.0" % q]], Hs[sl["HQ%d.0" % q]]
-                for ii in range(2):
-                    i = 2 * b + ii
-                    for g in range(2):
-                        mx(po[:, 256 * ii : 256 * ii + 256], hc[:, g, 128 * i : 128 * i + 128], hs[:, g, 128 * i : 128 * i + 128], w5c[:, 256 * g : 256 * g + 256], w5s[:, 256 * g : 256 * g + 256], g == 0, g == 1)
-            return run
+            tiles["o", q, b] = po = bank("px", 3)
+            hc, hs = tiles["Hc", q], tiles["Hs", q]
+            for ii in range(2):
+                i = 2 * b + ii
+                for g in range(2):
+                    mx(po[:, 256 * ii : 256 * ii + 256], hc[:, g, 128 * i : 128 * i + 128], hs[:, g, 128 * i : 128 * i + 128], w5c[:, 256 * g : 256 * g + 256], w5s[:, 256 * g : 256 * g + 256], g == 0, g == 1)
 
         def oe(q, b):
-            return lambda sl: nc.vector.tensor_tensor(
-                out=w2[sl["OE%d.0" % q]][:].rearrange("p (i n) -> p i n", i=4)[:, 2 * b : 2 * b + 2],
-                in0=bank["pv"][sl["O%d.%d" % (q, b)]][:].rearrange("p (i n) -> p i n", i=2),
+            if b == 0:
+                tiles["v", q] = ring([P, 1024], F32, "v", 7)
+            nc.vector.tensor_tensor(
+                out=tiles["v", q][:].rearrange("p (i n) -> p i n", i=4)[:, 2 * b : 2 * b + 2],
+                in0=tiles["o", q, b][:].rearrange("p (i n) -> p i n", i=2),
                 in1=b5bc[:].unsqueeze(1).to_broadcast([P, 2, HC]),
                 op=ALU.add,
             )
 
         def sig2(q):
-            return lambda sl: nc.scalar.activation(out=s2[sl["S2_%d" % q]][:], in_=w2[sl["OE%d.0" % q]][:], func=FN.Sigmoid, scale=-100.0)
+            tiles["s2", q] = big([P, 1024], F32)
+            nc.scalar.activation(out=tiles["s2", q][:], in_=tiles["v", q][:], func=FN.Sigmoid, scale=-100.0)
 
         def ln2(q):
-            return lambda sl: nc.scalar.activation(out=s2[sl["S2_%d" % q]][:], in_=s2[sl["S2_%d" % q]][:], func=FN.Ln, bias=dl[:], scale=1.0)
+            nc.scalar.activation(out=tiles["s2", q][:], in_=tiles["s2", q][:], func=FN.Ln, bias=dl[:], scale=1.0)
 
         def fin2(q):
-            return lambda sl: nc.vector.scalar_tensor_tensor(
-                out=s2[sl["S2_%d" % q]][:], in0=s2[sl["S2_%d" % q]][:], scalar=-0.01, in1=w2[sl["OE%d.0" % q]][:], op0=ALU.mult, op1=ALU.max
-            )
+            s = tiles["s2", q][:]
+            nc.vector.scalar_tensor_tensor(out=s, in0=s, scalar=-0.01, in1=tiles["v", q][:], op0=ALU.mult, op1=ALU.max)
 
         def store(q):
-            return lambda sl: nc.sync.dma_start(out=outv[:, 4 * q : 4 * q + 4, :], in_=s2[sl["S2_%d" % q]][:].rearrange("p (i n) -> p i n", i=4))
+            nc.sync.dma_start(out=outv[:, 4 * q : 4 * q + 4, :], in_=tiles["s2", q][:].rearrange("p (i n) -> p i n", i=4))
+
+        for k in range(4):
+            add(act, "W4E%d" % k, ["W4T%d" % k], w4e, k)
+        first = 0
+        for c, size in enumerate(CHUNKS + (0,)):
+            units = range(first, first + size)
+            first += size
+            for n in units:
+                for t in range(4):
+                    add(act, "S%d.%d" % (n, t), ["A%d.%d" % (n, t), "B4"], sig1, n, t)
+            for q in SECOND[c]:
+                add(act, "S2_%d" % q, ["OE%d.1" % q], sig2, q)
+            for n in units:
+                add(act, "L%d" % n, ["S%d.3" % n], ln1, n)
+            for q in SECOND[c]:
+                add(act, "L2_%d" % q, ["S2_%d" % q], ln2, q)
+        second = [q for c in SECOND for q in c]
 
         for q in range(NQ):
-            op("XC%d" % q, "DVE", 150, ["LX%d" % q, 3500 + 500 * (q // 2)], xcat(q))
-            for b in range(2):
-                op("T%d.%d" % (q, b), "PE", 260, ["XC%d" % q], xt(q, b), ring=("pv", ["XE%d.%d" % (q, b)]))
-                op("XE%d.%d" % (q, b), "DVE", 450, ["T%d.%d" % (q, b)], xe(q, b), ring=("xr", ["XS%d" % q]) if b == 0 else None)
-            op("XS%d" % q, "DVE", 450, ["XE%d.0" % q, "XE%d.1" % q], xscale(q), ring=("xg", ["XQ%d" % q]))
-            op("XQ%d" % q, "DVE", 470, ["XS%d" % q], xquant(q))
-            for j in range(8):
-                op("A%d.%d" % (q, j), "PE", 220, ["XQ%d" % q, "W4Q%d" % (j // 4)], l1a(q, j), ring=("pa", ["S1_%d.%d" % (q, j)]))
-                op("S1_%d.%d" % (q, j), "ACT", 472, ["A%d.%d" % (q, j), "B4"], sig1(q, j), ring=("S", ["PA%d.%d" % (q, j // 4)]) if j % 4 == 0 else None, fn="sig")
-            for k in range(8):
-                op("D%d.%d" % (q, k), "PE", 246, ["XQ%d" % q, "W4Q%d" % (k % 2)], l1d(q, k), ring=("pv", ["WG%d.%d" % (q, k)]))
-                op("WG%d.%d" % (q, k), "DVE", 480, ["D%d.%d" % (q, k), "B4"], wguard(q, k), ring=("Wg", ["MX%d.%d" % (q, k)]) if k < 2 else None)
-            for g in range(2):
-                op("L1_%d.%d" % (q, g), "ACT", 1725, ["S1_%d.%d" % (q, 4 * g + t) for t in range(4)], ln1(q, g), fn="ln")
-                op("PA%d.%d" % (q, g), "POOL", 2150, ["L1_%d.%d" % (q, g)], pscale(q, g), ring=("Ag", ["HQ%d.%d" % (q, g)]))
-                op("MX%d.%d" % (q, g), "DVE", 870, ["PA%d.%d" % (q, g)] + ["WG%d.%d" % (q, 2 * i + g) for i in range(4)], hmax(q, g))
-                op("HQ%d.%d" % (q, g), "DVE", 470, ["MX%d.%d" % (q, g)], hquant(q, g), ring=("Hc", ["O%d.0" % q, "O%d.1" % q]) if g == 0 else None)
-            for b in range(2):
-                op("O%d.%d" % (q, b), "PE", 444, ["HQ%d.0" % q, "HQ%d.1" % q, "W5Q"], l2(q, b), ring=("pv", ["OE%d.%d" % (q, b)]))
-                op("OE%d.%d" % (q, b), "DVE", 480, ["O%d.%d" % (q, b)], oe(q, b), ring=("w2", ["F2_%d" % q]) if b == 0 else None)
-            op("S2_%d" % q, "ACT", 872, ["OE%d.0" % q, "OE%d.1" % q], sig2(q), ring=("s2", ["ST%d" % q]), fn="sig")
-            op("L2_%d" % q, "ACT", 872, ["S2_%d" % q], ln2(q), fn="ln")
-            op("F2_%d" % q, "DVE", 900, ["L2_%d" % q], fin2(q))
-            op("ST%d" % q, "SP", 2200, ["F2_%d" % q], store(q))
+            add(gp, "XC%d" % q, ["LX%d" % q], xcat, q)
+        for n in range(16):
+            for t in range(4):
+                add(gp, "P%d.%d" % (n, t), ["L%d" % n, "B4"], base, n, t)
 
-        quads = [q for c in CHUNKS for q in c]
-        act = ["W4E%d" % k for k in range(4)]
-        second = []
-        pending = []
-        for c in CHUNKS:
-            now, pending = pending[:-1], pending[-1:] + list(c)
-            second += now
-            act += ["S1_%d.%d" % (q, j) for q in c for j in range(8)] + ["S2_%d" % q for q in now]
-            act += ["L1_%d.%d" % (q, g) for q in c for g in range(2)] + ["L2_%d" % q for q in now]
-        second += pending
-        act += ["S2_%d" % q for q in pending] + ["L2_%d" % q for q in pending]
-        queues = {
-            "SP": [["LX0", "LW0", "LW1"] + ["LX%d" % q for q in (1, 2)] + ["LW5"] + ["LX%d" % q for q in range(3, NQ)] + ["ST%d" % q for q in second]],
-            "ACT": [act],
-            "POOL": [["PA%d.%d" % (q, g) for q in quads for g in range(2)]],
-            "PE": [
-                ["A%d.%d" % (q, j) for q in quads for j in range(8)],
-                ["W4T%d" % k for k in range(4)],
-                ["O%d.%d" % (q, b) for q in quads for b in range(2)],
-                ["T%d.%d" % (q, b) for q in quads for b in range(2)],
-                ["W5T0", "W5T1"],
-                ["D%d.%d" % (q, k) for q in quads for k in range(8)],
-            ],
-            "DVE": [
-                ["B4", "W4Q0", "W4Q1"],
-                [n % (q, g) for q in quads for g in range(2) for n in ("MX%d.%d", "HQ%d.%d")],
-                ["OE%d.%d" % (q, b) for q in quads for b in range(2)],
-                [n for q in quads for n in ("XC%d" % q, "XE%d.0" % q, "XE%d.1" % q, "XS%d" % q, "XQ%d" % q)],
-                ["F2_%d" % q for q in second],
-                ["W5E0", "W5E1", "W5Q"],
-                ["WG%d.%d" % (q, k) for q in quads for k in range(8)],
-            ],
-        }
-        plan(ops, queues, lambda name, slot: ops[name]["run"](slot))
+        for b in range(2):
+            add(pe_t, "T0.%d" % b, ["XC0"], xt, 0, b)
+        for k in range(4):
+            add(pe_t, "W4T%d" % k, ["LW%d" % (k // 2)], w4t, k)
+        for q in range(1, NQ):
+            for b in range(2):
+                add(pe_t, "T%d.%d" % (q, b), ["XC%d" % q], xt, q, b)
+            if q == 4:
+                for g in range(2):
+                    add(pe_t, "W5T%d" % g, ["LW5"], w5t, g)
+        for n in range(16):
+            q, g = n // 2, n % 2
+            for t in range(4):
+                add(pe_a, "A%d.%d" % (n, t), ["XQ%d" % q, "W4Q%d" % g], l1a, n, t)
+            for i in range(4):
+                add(pe_d, "D%d.%d" % (n, i), ["XQ%d" % q, "W4Q%d" % g], l1d, n, i)
+        for q in range(NQ):
+            for b in range(2):
+                add(pe_o, "O%d.%d" % (q, b), ["HQ%d" % (2 * q + 1), "W5Q"], l2, q, b)
+
+        def dve_x(q):
+            for b in range(2):
+                add(dve, "XE%d.%d" % (q, b), ["T%d.%d" % (q, b)], xe, q, b)
+            add(dve, "XQ%d" % q, ["XE%d.1" % q], xq, q)
+
+        def dve_oe(q, b):
+            add(dve, "OE%d.%d" % (q, b), ["O%d.%d" % (q, b)], oe, q, b)
+
+        def dve_f2(q):
+            add(dve, "F2_%d" % q, ["L2_%d" % q], fin2, q)
+
+        dve_x(0)
+        add(dve, "B4", [], run_b4)
+        for h in range(2):
+            add(dve, "W4Q%d" % h, ["W4E%d" % (2 * h + 1)], w4q, h)
+        for q in range(1, NQ):
+            dve_x(q)
+            if q == 4:
+                for g in range(2):
+                    add(dve, "W5E%d" % g, ["W5T%d" % g], w5e, g)
+                add(dve, "W5Q", ["W5E1"], w5q)
+        for n in range(16):
+            for i in range(4):
+                add(dve, "C%d.%d" % (n, i), ["D%d.%d" % (n, i), "P%d.3" % n], hsum, n, i)
+                if i == 1 and n >= 2:
+                    dve_oe(n // 2 - 1, n % 2)
+            add(dve, "R%d" % n, ["C%d.3" % n], hrelu, n)
+            add(dve, "HQ%d" % n, ["R%d" % n], hquant, n)
+        dve_f2(second[0])
+        dve_oe(7, 0)
+        dve_f2(second[1])
+        dve_oe(7, 1)
+        for q in second[2:]:
+            dve_f2(q)
+        for q in second:
+            add(sp, "ST%d" % q, ["F2_%d" % q], store, q)
+
+        weave([sp, act, gp, dve, pe_t, pe_a, pe_d, pe_o])

@@ -206,6 +206,9 @@ def tile_implicitnet_pa_t_kernel(tc, h3, x_in, W4, b4, W5, b5, out):
 
         def base(n, t):
             j = 4 * (n % 2) + t
+            if t == 0:
+                tiles["H", n] = ring([P, 2048], BF16, "H", 2)
+                nc.gpsimd.memset(tiles["H", n][:, 0:2], 0.0)
             s = tiles["S", n][:, t, :]
             nc.gpsimd.tensor_scalar(out=s, in0=s, scalar1=-0.01, scalar2=b4f[:, j : j + 1], op0=ALU.mult, op1=ALU.add)
 
@@ -217,8 +220,6 @@ def tile_implicitnet_pa_t_kernel(tc, h3, x_in, W4, b4, W5, b5, out):
                 mx(pd[:, 128 * t : 128 * t + 128], w4c[:, 128 * j : 128 * j + 128], w4s[:, 128 * j : 128 * j + 128], xc[q][:, 128 * i : 128 * i + 128], xs[q][:, 128 * i : 128 * i + 128], True, True)
 
         def hsum(n, i):
-            if i == 0:
-                tiles["H", n] = ring([P, 2048], BF16, "H", 2)
             nc.vector.tensor_tensor(
                 out=tiles["H", n][:].rearrange("p (i r t) -> p i r t", i=4, t=4)[:, i],
                 in0=tiles["d", n, i][:].rearrange("p (t r) -> p r t", t=4),

@@ -207,7 +207,7 @@ def tile_implicitnet_pa_t_kernel(tc, h3, x_in, W4, b4, W5, b5, out):
         def base(n, t):
             j = 4 * (n % 2) + t
             if t == 0:
-                tiles["H", n] = ring([P, 2048], BF16, "H", 2)
+                tiles["H", n] = ring([P, 2048], BF16, "H", 3)
                 nc.gpsimd.memset(tiles["H", n][:, 0:2], 0.0)
             s = tiles["S", n][:, t, :]
             nc.gpsimd.tensor_scalar(out=s, in0=s, scalar1=-0.01, scalar2=b4f[:, j : j + 1], op0=ALU.mult, op1=ALU.add)
@@ -300,9 +300,8 @@ def tile_implicitnet_pa_t_kernel(tc, h3, x_in, W4, b4, W5, b5, out):
         for q in range(1, NQ):
             for b in range(2):
                 add(pe_t, "T%d.%d" % (q, b), ["XC%d" % q], xt, q, b)
-            if q == 4:
-                for g in range(2):
-                    add(pe_t, "W5T%d" % g, ["LW5"], w5t, g)
+        for g in range(2):
+            add(pe_t, "W5T%d" % g, ["LW5"], w5t, g)
         for n in range(16):
             q, g = n // 2, n % 2
             for t in range(4):
@@ -313,34 +312,49 @@ def tile_implicitnet_pa_t_kernel(tc, h3, x_in, W4, b4, W5, b5, out):
             for b in range(2):
                 add(pe_o, "O%d.%d" % (q, b), ["HQ%d" % (2 * q + 1), "W5Q"], l2, q, b)
 
-        def dve_x(q):
-            for b in range(2):
-                add(dve, "XE%d.%d" % (q, b), ["T%d.%d" % (q, b)], xe, q, b)
-            add(dve, "XQ%d" % q, ["XE%d.1" % q], xq, q)
-
         def dve_oe(q, b):
             add(dve, "OE%d.%d" % (q, b), ["O%d.%d" % (q, b)], oe, q, b)
 
         def dve_f2(q):
             add(dve, "F2_%d" % q, ["L2_%d" % q], fin2, q)
 
-        dve_x(0)
+        def dve_xe(q, b):
+            add(dve, "XE%d.%d" % (q, b), ["T%d.%d" % (q, b)], xe, q, b)
+
+        def dve_xq(q):
+            add(dve, "XQ%d" % q, ["XE%d.1" % q], xq, q)
+
+        def dve_hq(n):
+            add(dve, "HQ%d" % n, ["R%d" % n], hquant, n)
+
+        dve_xe(0, 0)
+        dve_xe(0, 1)
         add(dve, "B4", [], run_b4)
+        dve_xq(0)
         for h in range(2):
             add(dve, "W4Q%d" % h, ["W4E%d" % (2 * h + 1)], w4q, h)
-        for q in range(1, NQ):
-            dve_x(q)
-            if q == 4:
-                for g in range(2):
-                    add(dve, "W5E%d" % g, ["W5T%d" % g], w5e, g)
-                add(dve, "W5Q", ["W5E1"], w5q)
+        dve_xe(1, 0)
+        dve_xe(1, 1)
+        for q in range(2, NQ):
+            dve_xe(q, 0)
+            dve_xq(q - 1)
+            dve_xe(q, 1)
+        add(dve, "W5E0", ["W5T0"], w5e, 0)
+        dve_xq(NQ - 1)
+        add(dve, "W5E1", ["W5T1"], w5e, 1)
         for n in range(16):
             for i in range(4):
                 add(dve, "C%d.%d" % (n, i), ["D%d.%d" % (n, i), "P%d.3" % n], hsum, n, i)
-                if i == 1 and n >= 2:
-                    dve_oe(n // 2 - 1, n % 2)
+                if i == 1:
+                    if n == 0:
+                        add(dve, "W5Q", ["W5E1"], w5q)
+                    if n >= 3:
+                        dve_oe((n - 3) // 2, (n - 3) % 2)
+            if n:
+                dve_hq(n - 1)
             add(dve, "R%d" % n, ["C%d.3" % n], hrelu, n)
-            add(dve, "HQ%d" % n, ["R%d" % n], hquant, n)
+        dve_oe(6, 1)
+        dve_hq(15)
         dve_f2(second[0])
         dve_oe(7, 0)
         dve_f2(second[1])

@@ -11,7 +11,6 @@ U8 = mybir.dt.uint8
 FP8X4 = mybir.dt.float8_e4m3fn_x4
 ALU = mybir.AluOpType
 FN = mybir.ActivationFunctionType
-ENG = mybir.EngineType
 
 P = 128
 N_TOK, HA, HB, HC, DIN = 4096, 512, 1024, 256, 3
@@ -20,8 +19,9 @@ NG = N_TOK // P
 NQ = 8
 CUT = 496
 DELTA = 2.0 ** -62
-CHUNKS = (4, 6, 4, 2)
-SECOND = ((), (), (), (0, 1, 2), (3, 4, 5, 6, 7))
+CHUNKS = (8, 6, 2)
+SECOND = ((), (), (0, 1, 2, 3), (4, 5, 6, 7))
+NB = 4
 
 
 def weave(queues):
@@ -49,7 +49,7 @@ def tile_implicitnet_pa_t_kernel(tc, h3, x_in, W4, b4, W5, b5, out):
     with ExitStack() as ctx:
         pool = ctx.enter_context(tc.tile_pool(name="sb", bufs=1))
         psum = ctx.enter_context(tc.psum_pool(name="psum", bufs=1))
-        ctx.enter_context(tc.manual_schedule(engines={ENG.Activation, ENG.DVE, ENG.Pool, ENG.SP}))
+        ctx.enter_context(tc.manual_schedule())
 
         def keep(shape, dt, name):
             return pool.tile(shape, dt, name=name, align_bytes=64)
@@ -57,8 +57,8 @@ def tile_implicitnet_pa_t_kernel(tc, h3, x_in, W4, b4, W5, b5, out):
         def ring(shape, dt, tag, bufs):
             return pool.tile(shape, dt, name=tag, tag=tag, bufs=bufs, align_bytes=64)
 
-        def bank(tag, bufs):
-            return psum.tile([P, 512], F32, name=tag, tag=tag, bufs=bufs)
+        def bank(tag):
+            return psum.tile([P, 512], F32, name=tag, tag=tag, bufs=NB)
 
         def big(shape, dt):
             return ring(shape, dt, "S", 13)
@@ -98,8 +98,8 @@ def tile_implicitnet_pa_t_kernel(tc, h3, x_in, W4, b4, W5, b5, out):
         def mx(o, lw, ls, rw, rs, start, stop):
             nc.tensor.matmul_mx(out=o, lhsT=lw.bitcast(FP8X4), lhsT_scale=ls, rhs=rw.bitcast(FP8X4), rhs_scale=rs, start=start, stop=stop)
 
-        sp, act, gp, dve = [], [], [], []
-        pe_t, pe_a, pe_d, pe_o = [], [], [], []
+        sp, act, gp, dve, pe = [], [], [], [], []
+        feeds = []
 
         def add(queue, name, needs, run, *args):
             queue.append((name, needs, lambda: run(*args)))
@@ -130,7 +130,7 @@ def tile_implicitnet_pa_t_kernel(tc, h3, x_in, W4, b4, W5, b5, out):
             nc.vector.tensor_scalar(out=pb4[:], in0=b4b[:], scalar1=100.0, scalar2=None, op0=ALU.mult)
 
         def w4t(k):
-            tiles["w4t", k] = pt = bank("pd", 2)
+            tiles["w4t", k] = pt = bank("pv")
             for jj in range(2):
                 for u in range(2):
                     j = 2 * k + jj
@@ -148,7 +148,7 @@ def tile_implicitnet_pa_t_kernel(tc, h3, x_in, W4, b4, W5, b5, out):
             nc.vector.quantize_mx(out=w4c[:, 512 * h : 512 * h + 512].bitcast(FP8X4), scales=w4s[:, 512 * h : 512 * h + 512], in_=tiles["w4g"][:, 2048 * h : 2048 * h + 2048])
 
         def w5t(g):
-            tiles["w5t", g] = pt = bank("px", 3)
+            tiles["w5t", g] = pt = bank("pv")
             for a in range(2):
                 for u in range(2):
                     lo = 512 * a + 256 * g + u
@@ -170,7 +170,7 @@ def tile_implicitnet_pa_t_kernel(tc, h3, x_in, W4, b4, W5, b5, out):
             nc.gpsimd.tensor_copy(out=X[q][:, :, HA - DIN : HA], in_=xin[:].rearrange("p (g c) -> p g c", c=DIN)[:, 4 * q : 4 * q + 4, :])
 
         def xt(q, b):
-            tiles["xt", q, b] = pt = bank("px", 3)
+            tiles["xt", q, b] = pt = bank("pv")
             xw = X[q][:].rearrange("p g k -> p (g k)").bitcast(F32)
             for ii in range(2):
                 for u in range(2):
@@ -191,7 +191,7 @@ def tile_implicitnet_pa_t_kernel(tc, h3, x_in, W4, b4, W5, b5, out):
 
         def l1a(n, t):
             q, j = n // 2, 4 * (n % 2) + t
-            tiles["a", n, t] = pa = bank("pa", 3)
+            tiles["a", n, t] = pa = bank("pa")
             mx(pa[:], w4c[:, 128 * j : 128 * j + 128], w4s[:, 128 * j : 128 * j + 128], xc[q][:], xs[q][:], True, True)
 
         def sig1(n, t):
@@ -214,7 +214,7 @@ def tile_implicitnet_pa_t_kernel(tc, h3, x_in, W4, b4, W5, b5, out):
 
         def l1d(n, i):
             q, g = n // 2, n % 2
-            tiles["d", n, i] = pd = bank("pd", 2)
+            tiles["d", n, i] = pd = bank("pv")
             for t in range(4):
                 j = 4 * g + t
                 mx(pd[:, 128 * t : 128 * t + 128], w4c[:, 128 * j : 128 * j + 128], w4s[:, 128 * j : 128 * j + 128], xc[q][:, 128 * i : 128 * i + 128], xs[q][:, 128 * i : 128 * i + 128], True, True)
@@ -239,7 +239,7 @@ def tile_implicitnet_pa_t_kernel(tc, h3, x_in, W4, b4, W5, b5, out):
             nc.vector.quantize_mx(out=tiles["Hc", q][:, g, :].bitcast(FP8X4), scales=tiles["Hs", q][:, g, :], in_=tiles["H", n][:])
 
         def l2(q, b):
-            tiles["o", q, b] = po = bank("px", 3)
+            tiles["o", q, b] = po = bank("pv")
             hc, hs = tiles["Hc", q], tiles["Hs", q]
             for ii in range(2):
                 i = 2 * b + ii
@@ -293,32 +293,8 @@ def tile_implicitnet_pa_t_kernel(tc, h3, x_in, W4, b4, W5, b5, out):
             for t in range(4):
                 add(gp, "P%d.%d" % (n, t), ["L%d" % n, "B4"], base, n, t)
 
-        for b in range(2):
-            add(pe_t, "T0.%d" % b, ["XC0"], xt, 0, b)
-        for k in range(4):
-            add(pe_t, "W4T%d" % k, ["LW%d" % (k // 2)], w4t, k)
-        for q in range(1, NQ):
-            for b in range(2):
-                add(pe_t, "T%d.%d" % (q, b), ["XC%d" % q], xt, q, b)
-        for g in range(2):
-            add(pe_t, "W5T%d" % g, ["LW5"], w5t, g)
-        for n in range(16):
-            q, g = n // 2, n % 2
-            for t in range(4):
-                add(pe_a, "A%d.%d" % (n, t), ["XQ%d" % q, "W4Q%d" % g], l1a, n, t)
-            for i in range(4):
-                add(pe_d, "D%d.%d" % (n, i), ["XQ%d" % q, "W4Q%d" % g], l1d, n, i)
-        for q in range(NQ):
-            for b in range(2):
-                add(pe_o, "O%d.%d" % (q, b), ["HQ%d" % (2 * q + 1), "W5Q"], l2, q, b)
-
-        def dve_oe(q, b):
-            add(dve, "OE%d.%d" % (q, b), ["O%d.%d" % (q, b)], oe, q, b)
-
-        def dve_f2(q):
-            add(dve, "F2_%d" % q, ["L2_%d" % q], fin2, q)
-
         def dve_xe(q, b):
+            add(feeds, "T%d.%d" % (q, b), ["XC%d" % q], xt, q, b)
             add(dve, "XE%d.%d" % (q, b), ["T%d.%d" % (q, b)], xe, q, b)
 
         def dve_xq(q):
@@ -326,6 +302,17 @@ def tile_implicitnet_pa_t_kernel(tc, h3, x_in, W4, b4, W5, b5, out):
 
         def dve_hq(n):
             add(dve, "HQ%d" % n, ["R%d" % n], hquant, n)
+
+        def dve_w5e(g):
+            add(feeds, "W5T%d" % g, ["LW5"], w5t, g)
+            add(dve, "W5E%d" % g, ["W5T%d" % g], w5e, g)
+
+        def dve_oe(q, b):
+            add(feeds, "O%d.%d" % (q, b), ["HQ%d" % (2 * q + 1), "W5Q"], l2, q, b)
+            add(dve, "OE%d.%d" % (q, b), ["O%d.%d" % (q, b)], oe, q, b)
+
+        def dve_f2(q):
+            add(dve, "F2_%d" % q, ["L2_%d" % q], fin2, q)
 
         dve_xe(0, 0)
         dve_xe(0, 1)
@@ -339,11 +326,13 @@ def tile_implicitnet_pa_t_kernel(tc, h3, x_in, W4, b4, W5, b5, out):
             dve_xe(q, 0)
             dve_xq(q - 1)
             dve_xe(q, 1)
-        add(dve, "W5E0", ["W5T0"], w5e, 0)
+        dve_w5e(0)
         dve_xq(NQ - 1)
-        add(dve, "W5E1", ["W5T1"], w5e, 1)
+        dve_w5e(1)
+        prep = len(feeds)
         for n in range(16):
             for i in range(4):
+                add(feeds, "D%d.%d" % (n, i), ["XQ%d" % (n // 2), "W4Q%d" % (n % 2)], l1d, n, i)
                 add(dve, "C%d.%d" % (n, i), ["D%d.%d" % (n, i), "P%d.3" % n], hsum, n, i)
                 if i == 1:
                     if n == 0:
@@ -364,4 +353,36 @@ def tile_implicitnet_pa_t_kernel(tc, h3, x_in, W4, b4, W5, b5, out):
         for q in second:
             add(sp, "ST%d" % q, ["F2_%d" % q], store, q)
 
-        weave([sp, act, gp, dve, pe_t, pe_a, pe_d, pe_o])
+        starts = [sum(CHUNKS[:c]) for c in range(len(CHUNKS) + 1)]
+        first_layer = []
+        for c in range(len(CHUNKS)):
+            banks = []
+            for n in range(starts[c], starts[c + 1]):
+                for t in range(4):
+                    add(banks, "A%d.%d" % (n, t), ["XQ%d" % (n // 2), "W4Q%d" % (n % 2)], l1a, n, t)
+            first_layer.append(banks)
+        pe += feeds[:2]
+        for k in range(4):
+            add(pe, "W4T%d" % k, ["LW%d" % (k // 2)], w4t, k)
+        pe += feeds[2:4]
+        ahead = first_layer[0]
+        for f in feeds[4:prep]:
+            pe += ahead[:2] + [f]
+            ahead = ahead[2:]
+        pe += ahead
+        c = 1
+        pe += first_layer[1][:NB]
+        ahead = first_layer[1][NB:]
+        for f in feeds[prep:]:
+            pe.append(f)
+            name = f[0]
+            if c < len(CHUNKS) and name[0] == "D" and int(name[1:].split(".")[0]) >= starts[c - 1] + CHUNKS[c - 1] // 2:
+                pe += ahead[:2]
+                ahead = ahead[2:]
+                if not ahead:
+                    c += 1
+                    if c < len(CHUNKS):
+                        pe += first_layer[c][:NB]
+                        ahead = first_layer[c][NB:]
+
+        weave([sp, act, gp, dve, pe])

@@ -20,7 +20,8 @@ NQ = 8
 CUT = 496
 DELTA = 2.0 ** -62
 CHUNKS = (8, 6, 2)
-SECOND = ((), (), (0, 1, 2, 3), (4, 5, 6, 7))
+SECOND = ((), (), (0, 1, 2, 3, 4), (5, 6, 7))
+LATE = 12
 NB = 4
 
 
@@ -69,10 +70,13 @@ def tile_implicitnet_pa_t_kernel(tc, h3, x_in, W4, b4, W5, b5, out):
         b4b = keep([P, 8], BF16, "b4b")
         b4f = keep([P, 8], F32, "b4f")
         pb4 = keep([P, 8], F32, "pb4")
+        nb4 = keep([P, 8], F32, "nb4")
         b5bc = keep([P, HC], BF16, "b5bc")
         tail13 = keep([P, NG, 16], BF16, "tail13")
         xin = keep([P, NG * DIN], BF16, "xin")
-        X = [keep([P, 4, HA], BF16, "X%d" % q) for q in range(NQ)]
+        X = []
+        for q in range(NQ):
+            X.append(ring([P, 4, HA], BF16, "X", NQ))
         xc = [keep([P, 512], U32, "xc%d" % q) for q in range(NQ)]
         xs = [keep([P, 512], U8, "xs%d" % q) for q in range(NQ)]
         w4c = keep([P, HB], U32, "w4c")
@@ -82,12 +86,12 @@ def tile_implicitnet_pa_t_kernel(tc, h3, x_in, W4, b4, W5, b5, out):
 
         nc.vector.memset(dl[:], DELTA)
         make_identity(nc, ident[:])
+        nc.scalar.dma_start(out=tail13[:, 0:4, 0:13], in_=h3v[:, 0:4, CUT : HA - DIN])
         nc.scalar.dma_start(out=xin[:], in_=x_in.rearrange("(p g) c -> p (g c)", g=NG))
-        nc.scalar.dma_start(out=tail13[:, 0:8, 0:13], in_=h3v[:, 0:8, CUT : HA - DIN])
         nc.scalar.dma_start(out=b4b[:].rearrange("p (g t) -> p g t", g=2), in_=b4.rearrange("(g p t) -> p g t", g=2, t=4))
         nc.scalar.activation(out=warm[:], in_=dl[:], func=FN.Sigmoid)
-        for a in range(1, 4):
-            nc.scalar.dma_start(out=tail13[:, 8 * a : 8 * a + 8, 0:13], in_=h3v[:, 8 * a : 8 * a + 8, CUT : HA - DIN])
+        for lo, hi in ((4, 8), (8, 20), (20, 32)):
+            nc.scalar.dma_start(out=tail13[:, lo:hi, 0:13], in_=h3v[:, lo:hi, CUT : HA - DIN])
         nc.scalar.dma_start(out=b5bc[:], in_=b5.partition_broadcast(P))
 
         tiles = {}
@@ -128,6 +132,7 @@ def tile_implicitnet_pa_t_kernel(tc, h3, x_in, W4, b4, W5, b5, out):
         def run_b4():
             nc.vector.tensor_copy(out=b4f[:], in_=b4b[:])
             nc.vector.tensor_scalar(out=pb4[:], in0=b4b[:], scalar1=100.0, scalar2=None, op0=ALU.mult)
+            nc.vector.tensor_scalar(out=nb4[:], in0=b4b[:], scalar1=-100.0, scalar2=None, op0=ALU.mult)
 
         def w4t(k):
             tiles["w4t", k] = pt = bank("pv")
@@ -198,7 +203,8 @@ def tile_implicitnet_pa_t_kernel(tc, h3, x_in, W4, b4, W5, b5, out):
             j = 4 * (n % 2) + t
             if t == 0:
                 tiles["S", n] = big([P, 4, 512], F32)
-            nc.scalar.activation(out=tiles["S", n][:, t, :], in_=tiles["a", n, t][:], func=FN.Sigmoid, bias=pb4[:, j : j + 1], scale=100.0)
+            bias, scale = (pb4, 100.0) if n < LATE else (nb4, -100.0)
+            nc.scalar.activation(out=tiles["S", n][:, t, :], in_=tiles["a", n, t][:], func=FN.Sigmoid, bias=bias[:, j : j + 1], scale=scale)
 
         def ln1(n):
             s = tiles["S", n][:].rearrange("p t x -> p (t x)")
@@ -230,6 +236,28 @@ def tile_implicitnet_pa_t_kernel(tc, h3, x_in, W4, b4, W5, b5, out):
         def hrelu(n):
             h = tiles["H", n]
             nc.vector.tensor_scalar(out=h[:], in0=h[:], scalar1=0.0, scalar2=None, op0=ALU.max)
+
+        def guard(n, i):
+            g = n % 2
+            if i == 0:
+                tiles["G", n] = ring([P, 2048], BF16, "X", NQ)
+            nc.vector.tensor_tensor(
+                out=tiles["G", n][:].rearrange("p (i r t) -> p i r t", i=4, t=4)[:, i],
+                in0=tiles["d", n, i][:].rearrange("p (t r) -> p r t", t=4),
+                in1=b4f[:, 4 * g : 4 * g + 4].unsqueeze(1).to_broadcast([P, P, 4]),
+                op=ALU.add,
+            )
+
+        def hmax(n):
+            tiles["H", n] = ring([P, 2048], BF16, "H", 3)
+            nc.vector.scalar_tensor_tensor(
+                out=tiles["H", n][:].rearrange("p (x t) -> p x t", t=4),
+                in0=tiles["S", n][:].rearrange("p t x -> p x t"),
+                scalar=-0.01,
+                in1=tiles["G", n][:].rearrange("p (x t) -> p x t", t=4),
+                op0=ALU.mult,
+                op1=ALU.max,
+            )
 
         def hquant(n):
             q, g = n // 2, n % 2
@@ -289,7 +317,7 @@ def tile_implicitnet_pa_t_kernel(tc, h3, x_in, W4, b4, W5, b5, out):
 
         for q in range(NQ):
             add(gp, "XC%d" % q, ["LX%d" % q], xcat, q)
-        for n in range(16):
+        for n in range(LATE):
             for t in range(4):
                 add(gp, "P%d.%d" % (n, t), ["L%d" % n, "B4"], base, n, t)
 
@@ -316,10 +344,10 @@ def tile_implicitnet_pa_t_kernel(tc, h3, x_in, W4, b4, W5, b5, out):
 
         dve_xe(0, 0)
         dve_xe(0, 1)
-        add(dve, "B4", [], run_b4)
+        add(dve, "W4Q0", ["W4E1"], w4q, 0)
         dve_xq(0)
-        for h in range(2):
-            add(dve, "W4Q%d" % h, ["W4E%d" % (2 * h + 1)], w4q, h)
+        add(dve, "B4", [], run_b4)
+        add(dve, "W4Q1", ["W4E3"], w4q, 1)
         dve_xe(1, 0)
         dve_xe(1, 1)
         for q in range(2, NQ):
@@ -329,8 +357,12 @@ def tile_implicitnet_pa_t_kernel(tc, h3, x_in, W4, b4, W5, b5, out):
         dve_w5e(0)
         dve_xq(NQ - 1)
         dve_w5e(1)
+        for n in range(LATE, 16):
+            for i in range(4):
+                add(feeds, "D%d.%d" % (n, i), ["XQ%d" % (n // 2), "W4Q%d" % (n % 2)], l1d, n, i)
+                add(dve, "G%d.%d" % (n, i), ["D%d.%d" % (n, i)], guard, n, i)
         prep = len(feeds)
-        for n in range(16):
+        for n in range(LATE):
             for i in range(4):
                 add(feeds, "D%d.%d" % (n, i), ["XQ%d" % (n // 2), "W4Q%d" % (n % 2)], l1d, n, i)
                 add(dve, "C%d.%d" % (n, i), ["D%d.%d" % (n, i), "P%d.3" % n], hsum, n, i)
@@ -342,6 +374,10 @@ def tile_implicitnet_pa_t_kernel(tc, h3, x_in, W4, b4, W5, b5, out):
             if n:
                 dve_hq(n - 1)
             add(dve, "R%d" % n, ["C%d.3" % n], hrelu, n)
+        for n in range(LATE, 16):
+            dve_oe((n - 3) // 2, (n - 3) % 2)
+            add(dve, "R%d" % n, ["L%d" % n, "G%d.3" % n], hmax, n)
+            dve_hq(n - 1)
         dve_oe(6, 1)
         dve_hq(15)
         dve_f2(second[0])
@@ -361,9 +397,11 @@ def tile_implicitnet_pa_t_kernel(tc, h3, x_in, W4, b4, W5, b5, out):
                 for t in range(4):
                     add(banks, "A%d.%d" % (n, t), ["XQ%d" % (n // 2), "W4Q%d" % (n % 2)], l1a, n, t)
             first_layer.append(banks)
+        for k in (0, 1):
+            add(pe, "W4T%d" % k, ["LW0"], w4t, k)
         pe += feeds[:2]
-        for k in range(4):
-            add(pe, "W4T%d" % k, ["LW%d" % (k // 2)], w4t, k)
+        for k in (2, 3):
+            add(pe, "W4T%d" % k, ["LW1"], w4t, k)
         pe += feeds[2:4]
         ahead = first_layer[0]
         for f in feeds[4:prep]:
@@ -376,7 +414,9 @@ def tile_implicitnet_pa_t_kernel(tc, h3, x_in, W4, b4, W5, b5, out):
         for f in feeds[prep:]:
             pe.append(f)
             name = f[0]
-            if c < len(CHUNKS) and name[0] == "D" and int(name[1:].split(".")[0]) >= starts[c - 1] + CHUNKS[c - 1] // 2:
+            if name[0] == "D":
+                n, i = [int(s) for s in name[1:].split(".")]
+            if c < len(CHUNKS) and name[0] == "D" and 4 * n + i + 1 >= 4 * (starts[c - 1] + CHUNKS[c - 1] // 2):
                 pe += ahead[:2]
                 ahead = ahead[2:]
                 if not ahead:

@@ -227,9 +227,9 @@ def tile_implicitnet_pa_t_kernel(tc, h3, x_in, W4, b4, W5, b5, out):
 
         def hsum(n, i):
             nc.vector.tensor_tensor(
-                out=tiles["H", n][:].rearrange("p (i r t) -> p i r t", i=4, t=4)[:, i],
-                in0=tiles["d", n, i][:].rearrange("p (t r) -> p r t", t=4),
-                in1=tiles["S", n][:].rearrange("p t (i r) -> p i r t", i=4)[:, i],
+                out=tiles["H", n][:, 512 * i : 512 * i + 512].rearrange("p (c s t) -> p c t s", s=4, t=4),
+                in0=tiles["d", n, i][:].rearrange("p (t c s) -> p c t s", t=4, s=4),
+                in1=tiles["S", n][:, :, 128 * i : 128 * i + 128].rearrange("p t (c s) -> p c t s", s=4),
                 op=ALU.add,
             )
 

@@ -17,7 +17,7 @@ N_TOK, HA, HB, HC, DIN = 4096, 512, 1024, 256, 3
 FLOPS = 2 * N_TOK * HA * HB + 2 * N_TOK * HB * HC
 NG = N_TOK // P
 NQ = 8
-CUT = 496
+H3 = HA - DIN
 DELTA = 2.0 ** -62
 CHUNKS = (8, 6, 2)
 SECOND = ((), (), (0, 1, 2, 3, 4), (5, 6, 7))
@@ -72,7 +72,6 @@ def tile_implicitnet_pa_t_kernel(tc, h3, x_in, W4, b4, W5, b5, out):
         pb4 = keep([P, 8], F32, "pb4")
         nb4 = keep([P, 8], F32, "nb4")
         b5bc = keep([P, HC], BF16, "b5bc")
-        tail13 = keep([P, NG, 16], BF16, "tail13")
         xin = keep([P, NG * DIN], BF16, "xin")
         X = []
         for q in range(NQ):
@@ -86,13 +85,9 @@ def tile_implicitnet_pa_t_kernel(tc, h3, x_in, W4, b4, W5, b5, out):
 
         nc.vector.memset(dl[:], DELTA)
         make_identity(nc, ident[:])
-        nc.scalar.dma_start(out=tail13[:, 0:4, 0:13], in_=h3v[:, 0:4, CUT : HA - DIN])
         nc.scalar.dma_start(out=xin[:], in_=x_in.rearrange("(p g) c -> p (g c)", g=NG))
         nc.scalar.dma_start(out=b4b[:].rearrange("p (g t) -> p g t", g=2), in_=b4.rearrange("(g p t) -> p g t", g=2, t=4))
         nc.scalar.activation(out=warm[:], in_=dl[:], func=FN.Sigmoid)
-        for lo, hi in ((4, 8), (8, 20), (20, 32)):
-            nc.scalar.dma_start(out=tail13[:, lo:hi, 0:13], in_=h3v[:, lo:hi, CUT : HA - DIN])
-        nc.scalar.dma_start(out=b5bc[:], in_=b5.partition_broadcast(P))
 
         tiles = {}
 
@@ -109,7 +104,7 @@ def tile_implicitnet_pa_t_kernel(tc, h3, x_in, W4, b4, W5, b5, out):
             queue.append((name, needs, lambda: run(*args)))
 
         def ld_x(q):
-            nc.sync.dma_start(out=X[q][:, :, 0:CUT], in_=h3v[:, 4 * q : 4 * q + 4, 0:CUT])
+            nc.sync.dma_start(out=X[q][:, :, 0:H3], in_=h3v[:, 4 * q : 4 * q + 4, :])
 
         def ld_w4(h):
             if h == 0:
@@ -128,6 +123,7 @@ def tile_implicitnet_pa_t_kernel(tc, h3, x_in, W4, b4, W5, b5, out):
         add(sp, "LW5", [], ld_w5)
         for q in range(3, NQ):
             add(sp, "LX%d" % q, [], ld_x, q)
+        add(sp, "B5", [], lambda: nc.sync.dma_start(out=b5bc[:], in_=b5.partition_broadcast(P)))
 
         def run_b4():
             nc.vector.tensor_copy(out=b4f[:], in_=b4b[:])
@@ -171,8 +167,9 @@ def tile_implicitnet_pa_t_kernel(tc, h3, x_in, W4, b4, W5, b5, out):
             nc.vector.quantize_mx(out=w5c[:].bitcast(FP8X4), scales=w5s[:], in_=tiles["w5g"][:])
 
         def xcat(q):
-            nc.gpsimd.tensor_copy(out=X[q][:, :, CUT : HA - DIN], in_=tail13[:, 4 * q : 4 * q + 4, 0:13])
-            nc.gpsimd.tensor_copy(out=X[q][:, :, HA - DIN : HA], in_=xin[:].rearrange("p (g c) -> p g c", c=DIN)[:, 4 * q : 4 * q + 4, :])
+            last = X[q][:, :, H3 - 1 : H3]
+            nc.gpsimd.tensor_copy(out=last, in_=last)
+            nc.gpsimd.tensor_copy(out=X[q][:, :, H3:HA], in_=xin[:].rearrange("p (g c) -> p g c", c=DIN)[:, 4 * q : 4 * q + 4, :])
 
         def xt(q, b):
             tiles["xt", q, b] = pt = bank("pv")
@@ -276,27 +273,32 @@ def tile_implicitnet_pa_t_kernel(tc, h3, x_in, W4, b4, W5, b5, out):
 
         def oe(q, b):
             if b == 0:
-                tiles["v", q] = ring([P, 1024], F32, "v", 7)
+                tiles["v", q] = ring([P, 4, HC], F32, "v", 7)
             nc.vector.tensor_tensor(
-                out=tiles["v", q][:].rearrange("p (i n) -> p i n", i=4)[:, 2 * b : 2 * b + 2],
+                out=tiles["v", q][:, 2 * b : 2 * b + 2, :],
                 in0=tiles["o", q, b][:].rearrange("p (i n) -> p i n", i=2),
                 in1=b5bc[:].unsqueeze(1).to_broadcast([P, 2, HC]),
                 op=ALU.add,
             )
 
-        def sig2(q):
-            tiles["s2", q] = big([P, 1024], F32)
-            nc.scalar.activation(out=tiles["s2", q][:], in_=tiles["v", q][:], func=FN.Sigmoid, scale=-100.0)
+        def sig2(q, lo, hi):
+            if lo == 0:
+                tiles["s2", q] = big([P, 4, HC], F32)
+            nc.scalar.activation(out=tiles["s2", q][:, lo:hi, :], in_=tiles["v", q][:, lo:hi, :], func=FN.Sigmoid, scale=-100.0)
 
-        def ln2(q):
-            nc.scalar.activation(out=tiles["s2", q][:], in_=tiles["s2", q][:], func=FN.Ln, bias=dl[:], scale=1.0)
+        def ln2(q, lo, hi):
+            s = tiles["s2", q][:, lo:hi, :]
+            nc.scalar.activation(out=s, in_=s, func=FN.Ln, bias=dl[:], scale=1.0)
 
-        def fin2(q):
-            s = tiles["s2", q][:]
-            nc.vector.scalar_tensor_tensor(out=s, in0=s, scalar=-0.01, in1=tiles["v", q][:], op0=ALU.mult, op1=ALU.max)
+        def fin2(q, lo, hi):
+            s = tiles["s2", q][:, lo:hi, :]
+            nc.vector.scalar_tensor_tensor(out=s, in0=s, scalar=-0.01, in1=tiles["v", q][:, lo:hi, :], op0=ALU.mult, op1=ALU.max)
 
-        def store(q):
-            nc.sync.dma_start(out=outv[:, 4 * q : 4 * q + 4, :], in_=tiles["s2", q][:].rearrange("p (i n) -> p i n", i=4))
+        def store(q, lo, hi):
+            nc.sync.dma_start(out=outv[:, 4 * q + lo : 4 * q + hi, :], in_=tiles["s2", q][:, lo:hi, :])
+
+        def parts(q):
+            return ((0, 2), (2, 4)) if q == NQ - 1 else ((0, 4),)
 
         for k in range(4):
             add(act, "W4E%d" % k, ["W4T%d" % k], w4e, k)
@@ -308,11 +310,13 @@ def tile_implicitnet_pa_t_kernel(tc, h3, x_in, W4, b4, W5, b5, out):
                 for t in range(4):
                     add(act, "S%d.%d" % (n, t), ["A%d.%d" % (n, t), "B4"], sig1, n, t)
             for q in SECOND[c]:
-                add(act, "S2_%d" % q, ["OE%d.1" % q], sig2, q)
+                for lo, hi in parts(q):
+                    add(act, "S2_%d.%d" % (q, hi), ["OE%d.%d" % (q, hi // 2 - 1)], sig2, q, lo, hi)
             for n in units:
                 add(act, "L%d" % n, ["S%d.3" % n], ln1, n)
             for q in SECOND[c]:
-                add(act, "L2_%d" % q, ["S2_%d" % q], ln2, q)
+                for lo, hi in parts(q):
+                    add(act, "L2_%d.%d" % (q, hi), ["S2_%d.%d" % (q, hi)], ln2, q, lo, hi)
         second = [q for c in SECOND for q in c]
 
         for q in range(NQ):
@@ -337,10 +341,11 @@ def tile_implicitnet_pa_t_kernel(tc, h3, x_in, W4, b4, W5, b5, out):
 
         def dve_oe(q, b):
             add(feeds, "O%d.%d" % (q, b), ["HQ%d" % (2 * q + 1), "W5Q"], l2, q, b)
-            add(dve, "OE%d.%d" % (q, b), ["O%d.%d" % (q, b)], oe, q, b)
+            add(dve, "OE%d.%d" % (q, b), ["O%d.%d" % (q, b), "B5"], oe, q, b)
 
         def dve_f2(q):
-            add(dve, "F2_%d" % q, ["L2_%d" % q], fin2, q)
+            for lo, hi in parts(q):
+                add(dve, "F2_%d.%d" % (q, hi), ["L2_%d.%d" % (q, hi)], fin2, q, lo, hi)
 
         dve_xe(0, 0)
         dve_xe(0, 1)
@@ -387,7 +392,8 @@ def tile_implicitnet_pa_t_kernel(tc, h3, x_in, W4, b4, W5, b5, out):
         for q in second[2:]:
             dve_f2(q)
         for q in second:
-            add(sp, "ST%d" % q, ["F2_%d" % q], store, q)
+            for lo, hi in parts(q):
+                add(sp, "ST%d.%d" % (q, hi), ["F2_%d.%d" % (q, hi)], store, q, lo, hi)
 
         starts = [sum(CHUNKS[:c]) for c in range(len(CHUNKS) + 1)]
         first_layer = []

@@ -19,10 +19,11 @@ NG = N_TOK // P
 NQ = 8
 H3 = HA - DIN
 DELTA = 2.0 ** -62
-CHUNKS = (8, 6, 2)
-SECOND = ((), (), (0, 1, 2, 3, 4), (5, 6, 7))
+CHUNKS = (6, 6, 4)
+SECOND = ((), (), (0, 1, 2, 3), (4, 5, 6, 7))
 LATE = 12
 NB = 4
+LAG = 15
 
 
 def weave(queues):
@@ -245,23 +246,24 @@ def tile_implicitnet_pa_t_kernel(tc, h3, x_in, W4, b4, W5, b5, out):
                 op=ALU.add,
             )
 
-        def hmax(n):
-            tiles["H", n] = ring([P, 2048], BF16, "H", 3)
+        def hmax(n, lo, hi):
+            if lo == 0:
+                tiles["H", n] = ring([P, 2048], BF16, "H", 3)
             nc.vector.scalar_tensor_tensor(
-                out=tiles["H", n][:].rearrange("p (x t) -> p x t", t=4),
-                in0=tiles["S", n][:].rearrange("p t x -> p x t"),
+                out=tiles["H", n][:, 4 * lo : 4 * hi].rearrange("p (x t) -> p x t", t=4),
+                in0=tiles["S", n][:, :, lo:hi].rearrange("p t x -> p x t"),
                 scalar=-0.01,
-                in1=tiles["G", n][:].rearrange("p (x t) -> p x t", t=4),
+                in1=tiles["G", n][:, 4 * lo : 4 * hi].rearrange("p (x t) -> p x t", t=4),
                 op0=ALU.mult,
                 op1=ALU.max,
             )
 
-        def hquant(n):
+        def hquant(n, lo, hi):
             q, g = n // 2, n % 2
-            if g == 0:
+            if n % 2 == 0:
                 tiles["Hc", q] = ring([P, 2, 512], U32, "Hc", 2)
                 tiles["Hs", q] = ring([P, 2, 512], U8, "Hs", 2)
-            nc.vector.quantize_mx(out=tiles["Hc", q][:, g, :].bitcast(FP8X4), scales=tiles["Hs", q][:, g, :], in_=tiles["H", n][:])
+            nc.vector.quantize_mx(out=tiles["Hc", q][:, g, lo:hi].bitcast(FP8X4), scales=tiles["Hs", q][:, g, lo:hi], in_=tiles["H", n][:, 4 * lo : 4 * hi])
 
         def l2(q, b):
             tiles["o", q, b] = po = bank("pv")
@@ -273,7 +275,7 @@ def tile_implicitnet_pa_t_kernel(tc, h3, x_in, W4, b4, W5, b5, out):
 
         def oe(q, b):
             if b == 0:
-                tiles["v", q] = ring([P, 4, HC], F32, "v", 7)
+                tiles["v", q] = ring([P, 4, HC], F32, "v", 8)
             nc.vector.tensor_tensor(
                 out=tiles["v", q][:, 2 * b : 2 * b + 2, :],
                 in0=tiles["o", q, b][:].rearrange("p (i n) -> p i n", i=2),
@@ -332,15 +334,18 @@ def tile_implicitnet_pa_t_kernel(tc, h3, x_in, W4, b4, W5, b5, out):
         def dve_xq(q):
             add(dve, "XQ%d" % q, ["XE%d.1" % q], xq, q)
 
-        def dve_hq(n):
-            add(dve, "HQ%d" % n, ["R%d" % n], hquant, n)
+        def dve_hq(n, lo=0, hi=512):
+            add(dve, "HQ%d.%d" % (n, hi), ["R%d.%d" % (n, hi)], hquant, n, lo, hi)
+
+        def dve_max(n, lo=0, hi=512):
+            add(dve, "R%d.%d" % (n, hi), ["L%d" % n, "G%d.3" % n], hmax, n, lo, hi)
 
         def dve_w5e(g):
             add(feeds, "W5T%d" % g, ["LW5"], w5t, g)
             add(dve, "W5E%d" % g, ["W5T%d" % g], w5e, g)
 
         def dve_oe(q, b):
-            add(feeds, "O%d.%d" % (q, b), ["HQ%d" % (2 * q + 1), "W5Q"], l2, q, b)
+            add(feeds, "O%d.%d" % (q, b), ["HQ%d.%d" % (2 * q + 1, 256 * (b + 1) if q == NQ - 1 else 512), "W5Q"], l2, q, b)
             add(dve, "OE%d.%d" % (q, b), ["O%d.%d" % (q, b), "B5"], oe, q, b)
 
         def dve_f2(q):
@@ -378,18 +383,22 @@ def tile_implicitnet_pa_t_kernel(tc, h3, x_in, W4, b4, W5, b5, out):
                         dve_oe((n - 3) // 2, (n - 3) % 2)
             if n:
                 dve_hq(n - 1)
-            add(dve, "R%d" % n, ["C%d.3" % n], hrelu, n)
-        for n in range(LATE, 16):
+            add(dve, "R%d.512" % n, ["C%d.3" % n], hrelu, n)
+        for n in range(LATE, 15):
+            dve_max(n)
             dve_oe((n - 3) // 2, (n - 3) % 2)
-            add(dve, "R%d" % n, ["L%d" % n, "G%d.3" % n], hmax, n)
             dve_hq(n - 1)
+        dve_max(15, 0, 256)
+        dve_hq(14)
+        dve_oe(6, 0)
+        dve_hq(15, 0, 256)
+        dve_max(15, 256, 512)
         dve_oe(6, 1)
-        dve_hq(15)
-        dve_f2(second[0])
+        dve_hq(15, 256, 512)
         dve_oe(7, 0)
-        dve_f2(second[1])
+        dve_f2(second[0])
         dve_oe(7, 1)
-        for q in second[2:]:
+        for q in second[1:]:
             dve_f2(q)
         for q in second:
             for lo, hi in parts(q):
@@ -422,7 +431,7 @@ def tile_implicitnet_pa_t_kernel(tc, h3, x_in, W4, b4, W5, b5, out):
             name = f[0]
             if name[0] == "D":
                 n, i = [int(s) for s in name[1:].split(".")]
-            if c < len(CHUNKS) and name[0] == "D" and 4 * n + i + 1 >= 4 * (starts[c - 1] + CHUNKS[c - 1] // 2):
+            if c < len(CHUNKS) and name[0] == "D" and 4 * n + i >= 4 * starts[c] - LAG:
                 pe += ahead[:2]
                 ahead = ahead[2:]
                 if not ahead:

@@ -246,17 +246,18 @@ def tile_implicitnet_pa_t_kernel(tc, h3, x_in, W4, b4, W5, b5, out):
                 op=ALU.add,
             )
 
-        def hmax(n, lo, hi):
+        def hscale(n, lo, hi):
             if lo == 0:
                 tiles["H", n] = ring([P, 2048], BF16, "H", 3)
-            nc.vector.scalar_tensor_tensor(
-                out=tiles["H", n][:, 4 * lo : 4 * hi].rearrange("p (x t) -> p x t", t=4),
-                in0=tiles["S", n][:, :, lo:hi].rearrange("p t x -> p x t"),
-                scalar=-0.01,
-                in1=tiles["G", n][:, 4 * lo : 4 * hi].rearrange("p (x t) -> p x t", t=4),
-                op0=ALU.mult,
-                op1=ALU.max,
+            nc.vector.tensor_scalar(
+                out=tiles["H", n][:, 4 * lo : 4 * hi].rearrange("p (c s t) -> p c t s", s=4, t=4),
+                in0=tiles["S", n][:, :, lo:hi].rearrange("p t (c s) -> p c t s", s=4),
+                scalar1=-0.01, scalar2=None, op0=ALU.mult,
             )
+
+        def hmax(n, lo, hi):
+            h = tiles["H", n][:, 4 * lo : 4 * hi]
+            nc.vector.tensor_tensor(out=h, in0=h, in1=tiles["G", n][:, 4 * lo : 4 * hi], op=ALU.max)
 
         def hquant(n, lo, hi):
             q, g = n // 2, n % 2
@@ -337,8 +338,11 @@ def tile_implicitnet_pa_t_kernel(tc, h3, x_in, W4, b4, W5, b5, out):
         def dve_hq(n, lo=0, hi=512):
             add(dve, "HQ%d.%d" % (n, hi), ["R%d.%d" % (n, hi)], hquant, n, lo, hi)
 
+        def dve_scale(n, lo=0, hi=512):
+            add(dve, "M%d.%d" % (n, hi), ["L%d" % n], hscale, n, lo, hi)
+
         def dve_max(n, lo=0, hi=512):
-            add(dve, "R%d.%d" % (n, hi), ["L%d" % n, "G%d.3" % n], hmax, n, lo, hi)
+            add(dve, "R%d.%d" % (n, hi), ["M%d.%d" % (n, hi), "G%d.3" % n], hmax, n, lo, hi)
 
         def dve_w5e(g):
             add(feeds, "W5T%d" % g, ["LW5"], w5t, g)
@@ -385,13 +389,16 @@ def tile_implicitnet_pa_t_kernel(tc, h3, x_in, W4, b4, W5, b5, out):
                 dve_hq(n - 1)
             add(dve, "R%d.512" % n, ["C%d.3" % n], hrelu, n)
         for n in range(LATE, 15):
-            dve_max(n)
+            dve_scale(n)
             dve_oe((n - 3) // 2, (n - 3) % 2)
             dve_hq(n - 1)
-        dve_max(15, 0, 256)
+            dve_max(n)
+        dve_scale(15, 0, 256)
         dve_hq(14)
-        dve_oe(6, 0)
+        dve_max(15, 0, 256)
+        dve_scale(15, 256, 512)
         dve_hq(15, 0, 256)
+        dve_oe(6, 0)
         dve_max(15, 256, 512)
         dve_oe(6, 1)
         dve_hq(15, 256, 512)

@@ -19,11 +19,20 @@ NG = N_TOK // P
 NQ = 8
 H3 = HA - DIN
 DELTA = 2.0 ** -62
-CHUNKS = (6, 6, 4)
+NU = 16
+CHUNKS = (7, 5, 4)
 SECOND = ((), (), (0, 1, 2, 3), (4, 5, 6, 7))
-LATE = 12
+GUARD = (12, 13, 14, 15)
+EARLY = 14
+STARTS = (12, 43)
+RATE0 = (2, 1)
+RATEG = (4, 3)
+RATE = (4, 3)
+OPOS = 3
+HQD = 3
+RP = 1
+PREF = 3
 NB = 4
-LAG = 15
 
 
 def weave(queues):
@@ -146,8 +155,8 @@ def tile_implicitnet_pa_t_kernel(tc, h3, x_in, W4, b4, W5, b5, out):
                 in_=tiles["w4t", k][:].rearrange("p (j u m) -> p j m u", j=2, u=2),
             )
 
-        def w4q(h):
-            nc.vector.quantize_mx(out=w4c[:, 512 * h : 512 * h + 512].bitcast(FP8X4), scales=w4s[:, 512 * h : 512 * h + 512], in_=tiles["w4g"][:, 2048 * h : 2048 * h + 2048])
+        def w4q(lo, hi):
+            nc.vector.quantize_mx(out=w4c[:, 128 * lo : 128 * hi].bitcast(FP8X4), scales=w4s[:, 128 * lo : 128 * hi], in_=tiles["w4g"][:, 512 * lo : 512 * hi])
 
         def w5t(g):
             tiles["w5t", g] = pt = bank("pv")
@@ -201,18 +210,25 @@ def tile_implicitnet_pa_t_kernel(tc, h3, x_in, W4, b4, W5, b5, out):
             j = 4 * (n % 2) + t
             if t == 0:
                 tiles["S", n] = big([P, 4, 512], F32)
-            bias, scale = (pb4, 100.0) if n < LATE else (nb4, -100.0)
+            bias, scale = (pb4, 100.0) if n not in GUARD else (nb4, -100.0)
             nc.scalar.activation(out=tiles["S", n][:, t, :], in_=tiles["a", n, t][:], func=FN.Sigmoid, bias=bias[:, j : j + 1], scale=scale)
 
         def ln1(n):
             s = tiles["S", n][:].rearrange("p t x -> p (t x)")
             nc.scalar.activation(out=s, in_=s, func=FN.Ln, bias=dl[:], scale=1.0)
 
+        def htile(n):
+            if ("H", n // 2) not in tiles:
+                tiles["H", n // 2] = ring([P, 2, 2048], BF16, "H", 2)
+            return tiles["H", n // 2][:, n % 2, :]
+
+        def hview(n):
+            return tiles["H", n // 2][:, n % 2, :]
+
         def base(n, t):
             j = 4 * (n % 2) + t
             if t == 0:
-                tiles["H", n] = ring([P, 2048], BF16, "H", 3)
-                nc.gpsimd.memset(tiles["H", n][:, 0:2], 0.0)
+                nc.gpsimd.memset(htile(n)[:, 0:2], 0.0)
             s = tiles["S", n][:, t, :]
             nc.gpsimd.tensor_scalar(out=s, in0=s, scalar1=-0.01, scalar2=b4f[:, j : j + 1], op0=ALU.mult, op1=ALU.add)
 
@@ -225,15 +241,15 @@ def tile_implicitnet_pa_t_kernel(tc, h3, x_in, W4, b4, W5, b5, out):
 
         def hsum(n, i):
             nc.vector.tensor_tensor(
-                out=tiles["H", n][:, 512 * i : 512 * i + 512].rearrange("p (c s t) -> p c t s", s=4, t=4),
+                out=hview(n)[:, 512 * i : 512 * i + 512].rearrange("p (c s t) -> p c t s", s=4, t=4),
                 in0=tiles["d", n, i][:].rearrange("p (t c s) -> p c t s", t=4, s=4),
                 in1=tiles["S", n][:, :, 128 * i : 128 * i + 128].rearrange("p t (c s) -> p c t s", s=4),
                 op=ALU.add,
             )
 
-        def hrelu(n):
-            h = tiles["H", n]
-            nc.vector.tensor_scalar(out=h[:], in0=h[:], scalar1=0.0, scalar2=None, op0=ALU.max)
+        def hrelu(n, lo, hi):
+            h = hview(n)[:, 4 * lo : 4 * hi]
+            nc.vector.tensor_scalar(out=h, in0=h, scalar1=0.0, scalar2=None, op0=ALU.max)
 
         def guard(n, i):
             g = n % 2
@@ -246,25 +262,37 @@ def tile_implicitnet_pa_t_kernel(tc, h3, x_in, W4, b4, W5, b5, out):
                 op=ALU.add,
             )
 
+        def hrelu2(q):
+            h = tiles["H", q][:].rearrange("p g x -> p (g x)")
+            nc.vector.tensor_scalar(out=h, in0=h, scalar1=0.0, scalar2=None, op0=ALU.max)
+
+        def hnone():
+            pass
+
         def hscale(n, lo, hi):
-            if lo == 0:
-                tiles["H", n] = ring([P, 2048], BF16, "H", 3)
+            h = htile(n) if lo == 0 else hview(n)
             nc.vector.tensor_scalar(
-                out=tiles["H", n][:, 4 * lo : 4 * hi].rearrange("p (c s t) -> p c t s", s=4, t=4),
+                out=h[:, 4 * lo : 4 * hi].rearrange("p (c s t) -> p c t s", s=4, t=4),
                 in0=tiles["S", n][:, :, lo:hi].rearrange("p t (c s) -> p c t s", s=4),
                 scalar1=-0.01, scalar2=None, op0=ALU.mult,
             )
 
         def hmax(n, lo, hi):
-            h = tiles["H", n][:, 4 * lo : 4 * hi]
+            h = hview(n)[:, 4 * lo : 4 * hi]
             nc.vector.tensor_tensor(out=h, in0=h, in1=tiles["G", n][:, 4 * lo : 4 * hi], op=ALU.max)
 
-        def hquant(n, lo, hi):
-            q, g = n // 2, n % 2
-            if n % 2 == 0:
+        def hquant(q, g0, g1, lo, hi):
+            if g0 == 0 and lo == 0:
                 tiles["Hc", q] = ring([P, 2, 512], U32, "Hc", 2)
                 tiles["Hs", q] = ring([P, 2, 512], U8, "Hs", 2)
-            nc.vector.quantize_mx(out=tiles["Hc", q][:, g, lo:hi].bitcast(FP8X4), scales=tiles["Hs", q][:, g, lo:hi], in_=tiles["H", n][:, 4 * lo : 4 * hi])
+            if g1 - g0 == 2:
+                nc.vector.quantize_mx(
+                    out=tiles["Hc", q][:].rearrange("p g x -> p (g x)").bitcast(FP8X4),
+                    scales=tiles["Hs", q][:].rearrange("p g x -> p (g x)"),
+                    in_=tiles["H", q][:].rearrange("p g x -> p (g x)"),
+                )
+            else:
+                nc.vector.quantize_mx(out=tiles["Hc", q][:, g0, lo:hi].bitcast(FP8X4), scales=tiles["Hs", q][:, g0, lo:hi], in_=tiles["H", q][:, g0, 4 * lo : 4 * hi])
 
         def l2(q, b):
             tiles["o", q, b] = po = bank("pv")
@@ -305,26 +333,41 @@ def tile_implicitnet_pa_t_kernel(tc, h3, x_in, W4, b4, W5, b5, out):
 
         for k in range(4):
             add(act, "W4E%d" % k, ["W4T%d" % k], w4e, k)
+
+        def act_sig1(n):
+            for t in range(4):
+                add(act, "S%d.%d" % (n, t), ["A%d.%d" % (n, t), "B4"], sig1, n, t)
+
+        def act_ln1(n):
+            add(act, "L%d" % n, ["S%d.3" % n], ln1, n)
+
+        def act_sig2(q):
+            for lo, hi in parts(q):
+                add(act, "S2_%d.%d" % (q, hi), ["OE%d.%d" % (q, hi // 2 - 1)], sig2, q, lo, hi)
+
+        def act_ln2(q):
+            for lo, hi in parts(q):
+                add(act, "L2_%d.%d" % (q, hi), ["S2_%d.%d" % (q, hi)], ln2, q, lo, hi)
+
         first = 0
         for c, size in enumerate(CHUNKS + (0,)):
             units = range(first, first + size)
             first += size
             for n in units:
-                for t in range(4):
-                    add(act, "S%d.%d" % (n, t), ["A%d.%d" % (n, t), "B4"], sig1, n, t)
+                act_sig1(n)
             for q in SECOND[c]:
-                for lo, hi in parts(q):
-                    add(act, "S2_%d.%d" % (q, hi), ["OE%d.%d" % (q, hi // 2 - 1)], sig2, q, lo, hi)
+                act_sig2(q)
             for n in units:
-                add(act, "L%d" % n, ["S%d.3" % n], ln1, n)
+                act_ln1(n)
             for q in SECOND[c]:
-                for lo, hi in parts(q):
-                    add(act, "L2_%d.%d" % (q, hi), ["S2_%d.%d" % (q, hi)], ln2, q, lo, hi)
+                act_ln2(q)
         second = [q for c in SECOND for q in c]
 
         for q in range(NQ):
             add(gp, "XC%d" % q, ["LX%d" % q], xcat, q)
-        for n in range(LATE):
+        for n in range(NU):
+            if n in GUARD:
+                continue
             for t in range(4):
                 add(gp, "P%d.%d" % (n, t), ["L%d" % n, "B4"], base, n, t)
 
@@ -335,8 +378,11 @@ def tile_implicitnet_pa_t_kernel(tc, h3, x_in, W4, b4, W5, b5, out):
         def dve_xq(q):
             add(dve, "XQ%d" % q, ["XE%d.1" % q], xq, q)
 
-        def dve_hq(n, lo=0, hi=512):
-            add(dve, "HQ%d.%d" % (n, hi), ["R%d.%d" % (n, hi)], hquant, n, lo, hi)
+        def dve_hq2(q):
+            add(dve, "HQ%d" % q, ["R%d.512" % (2 * q + 1), "R%d.512" % (2 * q)], hquant, q, 0, 2, 0, 512)
+
+        def dve_hq1(n, lo=0, hi=512):
+            add(dve, "HQ%d.%d" % (n, hi), ["R%d.%d" % (n, hi)], hquant, n // 2, n % 2, n % 2 + 1, lo, hi)
 
         def dve_scale(n, lo=0, hi=512):
             add(dve, "M%d.%d" % (n, hi), ["L%d" % n], hscale, n, lo, hi)
@@ -348,20 +394,27 @@ def tile_implicitnet_pa_t_kernel(tc, h3, x_in, W4, b4, W5, b5, out):
             add(feeds, "W5T%d" % g, ["LW5"], w5t, g)
             add(dve, "W5E%d" % g, ["W5T%d" % g], w5e, g)
 
-        def dve_oe(q, b):
-            add(feeds, "O%d.%d" % (q, b), ["HQ%d.%d" % (2 * q + 1, 256 * (b + 1) if q == NQ - 1 else 512), "W5Q"], l2, q, b)
+        def dve_oe(k):
+            q, b = k // 2, k % 2
+            add(feeds, "O%d.%d" % (q, b), ["HQ15.%d" % (256 * (b + 1)) if q == NQ - 1 else "HQ%d" % q, "W5Q"], l2, q, b)
             add(dve, "OE%d.%d" % (q, b), ["O%d.%d" % (q, b), "B5"], oe, q, b)
 
         def dve_f2(q):
             for lo, hi in parts(q):
                 add(dve, "F2_%d.%d" % (q, hi), ["L2_%d.%d" % (q, hi)], fin2, q, lo, hi)
 
+        def dve_guard(k):
+            n, i = GUARD[k // 4], k % 4
+            add(feeds, "D%d.%d" % (n, i), ["XQ%d" % (n // 2), "W4Q%d" % (3 if n % 2 else 1)], l1d, n, i)
+            add(dve, "G%d.%d" % (n, i), ["D%d.%d" % (n, i)], guard, n, i)
+
         dve_xe(0, 0)
         dve_xe(0, 1)
-        add(dve, "W4Q0", ["W4E1"], w4q, 0)
-        dve_xq(0)
         add(dve, "B4", [], run_b4)
-        add(dve, "W4Q1", ["W4E3"], w4q, 1)
+        dve_xq(0)
+        add(dve, "W4Q0", ["W4E0"], w4q, 0, 2)
+        add(dve, "W4Q1", ["W4E1"], w4q, 2, 4)
+        add(dve, "W4Q3", ["W4E3"], w4q, 4, 8)
         dve_xe(1, 0)
         dve_xe(1, 1)
         for q in range(2, NQ):
@@ -371,80 +424,156 @@ def tile_implicitnet_pa_t_kernel(tc, h3, x_in, W4, b4, W5, b5, out):
         dve_w5e(0)
         dve_xq(NQ - 1)
         dve_w5e(1)
-        for n in range(LATE, 16):
-            for i in range(4):
-                add(feeds, "D%d.%d" % (n, i), ["XQ%d" % (n // 2), "W4Q%d" % (n % 2)], l1d, n, i)
-                add(dve, "G%d.%d" % (n, i), ["D%d.%d" % (n, i)], guard, n, i)
         prep = len(feeds)
-        for n in range(LATE):
-            for i in range(4):
-                add(feeds, "D%d.%d" % (n, i), ["XQ%d" % (n // 2), "W4Q%d" % (n % 2)], l1d, n, i)
-                add(dve, "C%d.%d" % (n, i), ["D%d.%d" % (n, i), "P%d.3" % n], hsum, n, i)
-                if i == 1:
-                    if n == 0:
-                        add(dve, "W5Q", ["W5E1"], w5q)
-                    if n >= 3:
-                        dve_oe((n - 3) // 2, (n - 3) % 2)
-            if n:
-                dve_hq(n - 1)
-            add(dve, "R%d.512" % n, ["C%d.3" % n], hrelu, n)
-        for n in range(LATE, 15):
-            dve_scale(n)
-            dve_oe((n - 3) // 2, (n - 3) % 2)
-            dve_hq(n - 1)
-            dve_max(n)
-        dve_scale(15, 0, 256)
-        dve_hq(14)
-        dve_max(15, 0, 256)
-        dve_scale(15, 256, 512)
-        dve_hq(15, 0, 256)
-        dve_oe(6, 0)
-        dve_max(15, 256, 512)
-        dve_oe(6, 1)
-        dve_hq(15, 256, 512)
-        dve_oe(7, 0)
+        guards = 4 * len(GUARD)
+        for k in range(EARLY):
+            dve_guard(k)
+        add(dve, "W5Q", ["W5E1"], w5q)
+        state = {"g": EARLY, "o": 0}
+        cfeed = len(feeds)
+
+        pend = []
+
+        def hq_now():
+            while pend:
+                dve_hq2(pend.pop(0))
+
+        def flush(n):
+            for c in range(1, len(CHUNKS)):
+                if CHUNKS[c] and n == sum(CHUNKS[:c]):
+                    for q in SECOND[c]:
+                        hq_now()
+                        while state["o"] < 2 * q + 2:
+                            dve_oe(state["o"])
+                            state["o"] += 1
+
+        def some_oe(n, done):
+            if state["o"] < 14 and state["o"] // 2 < done:
+                dve_oe(state["o"])
+                state["o"] += 1
+
+        def some_guard(n):
+            left = sum(1 for m in range(n, NU) if m not in GUARD and m < GUARD[-1])
+            more = guards - state["g"] if left < 2 else (guards - state["g"]) // left
+            if n < GUARD[0]:
+                for k in range(state["g"], state["g"] + more):
+                    dve_guard(k)
+                state["g"] += more
+
+        def dve_c(n, i):
+            add(feeds, "D%d.%d" % (n, i), ["XQ%d" % (n // 2), "W4Q%d" % (3 if n % 2 else 1)], l1d, n, i)
+            add(dve, "C%d.%d" % (n, i), ["D%d.%d" % (n, i), "P%d.3" % n], hsum, n, i)
+
+        def dve_relu(n, lo, hi):
+            add(dve, "R%d.%d" % (n, hi), ["C%d.%d" % (n, hi // 128 - 1)], hrelu, n, lo, hi)
+
+        done = 0
+        unit_at = {}
+        for n in range(NU - 1):
+            flush(n)
+            unit_at[n] = len(feeds)
+            if n in GUARD:
+                if state["g"] < 4 * GUARD.index(n) + 4:
+                    for k in range(state["g"], 4 * GUARD.index(n) + 4):
+                        dve_guard(k)
+                    state["g"] = 4 * GUARD.index(n) + 4
+                dve_scale(n)
+                some_oe(n, done)
+                if pend:
+                    hq_now()
+                    done += 1
+                dve_max(n)
+            else:
+                for i in range(4):
+                    dve_c(n, i)
+                    if i == OPOS:
+                        some_oe(n, done)
+                    if i == HQD and pend:
+                        hq_now()
+                        done += 1
+                some_guard(n)
+                if RP and n < 14 and n // 2 * 2 not in GUARD and n // 2 * 2 + 1 not in GUARD:
+                    if n % 2:
+                        add(dve, "R%d.512" % n, ["C%d.3" % n, "C%d.3" % (n - 1)], hrelu2, n // 2)
+                        add(dve, "R%d.512" % (n - 1), [], hnone)
+                else:
+                    dve_relu(n, 0, 512)
+            if n % 2:
+                pend.append(n // 2)
+        hq_now()
+        if 15 in GUARD:
+            dve_scale(15, 0, 256)
+            dve_hq1(14)
+            dve_max(15, 0, 256)
+            dve_scale(15, 256, 512)
+            dve_hq1(15, 0, 256)
+            while state["o"] < 13:
+                dve_oe(state["o"])
+                state["o"] += 1
+            dve_max(15, 256, 512)
+        else:
+            dve_c(15, 0)
+            dve_c(15, 1)
+            dve_hq1(14)
+            dve_relu(15, 0, 256)
+            dve_c(15, 2)
+            dve_hq1(15, 0, 256)
+            dve_c(15, 3)
+            while state["o"] < 13:
+                dve_oe(state["o"])
+                state["o"] += 1
+            dve_relu(15, 256, 512)
+        dve_oe(13)
+        dve_hq1(15, 256, 512)
+        dve_oe(14)
         dve_f2(second[0])
-        dve_oe(7, 1)
+        dve_oe(15)
         for q in second[1:]:
             dve_f2(q)
         for q in second:
             for lo, hi in parts(q):
                 add(sp, "ST%d.%d" % (q, hi), ["F2_%d.%d" % (q, hi)], store, q, lo, hi)
 
-        starts = [sum(CHUNKS[:c]) for c in range(len(CHUNKS) + 1)]
-        first_layer = []
-        for c in range(len(CHUNKS)):
-            banks = []
-            for n in range(starts[c], starts[c + 1]):
-                for t in range(4):
-                    add(banks, "A%d.%d" % (n, t), ["XQ%d" % (n // 2), "W4Q%d" % (n % 2)], l1a, n, t)
-            first_layer.append(banks)
+        banks = []
+        for n in range(NU):
+            for t in range(4):
+                add(banks, "A%d.%d" % (n, t), ["XQ%d" % (n // 2), "W4Q%d" % (3 if n % 2 else t // 2)], l1a, n, t)
+        pe += feeds[:2]
         for k in (0, 1):
             add(pe, "W4T%d" % k, ["LW0"], w4t, k)
-        pe += feeds[:2]
         for k in (2, 3):
             add(pe, "W4T%d" % k, ["LW1"], w4t, k)
-        pe += feeds[2:4]
-        ahead = first_layer[0]
-        for f in feeds[4:prep]:
-            pe += ahead[:2] + [f]
-            ahead = ahead[2:]
-        pe += ahead
-        c = 1
-        pe += first_layer[1][:NB]
-        ahead = first_layer[1][NB:]
-        for f in feeds[prep:]:
+        pe += banks[:2] + feeds[2:3] + banks[2:4] + feeds[3:4]
+        ends = [4 * sum(CHUNKS[: c + 1]) for c in range(len(CHUNKS)) if CHUNKS[c]]
+        c = 0
+        a = 4
+        turn = 0
+        wait = 0
+        for k, f in enumerate(feeds[4:]):
+            k += 4
+            if c < len(ends):
+                start = 4 if c == 0 else ends[c - 1]
+                if c == 0 or k >= cfeed + STARTS[c - 1]:
+                    while c and a < start + NB:
+                        pe.append(banks[a])
+                        a += 1
+                    rate = (RATE0 if k < prep else RATEG) if c == 0 else RATE
+                    turn += rate[0]
+                    while turn >= rate[1] and a < ends[c]:
+                        pe.append(banks[a])
+                        a += 1
+                        turn -= rate[1]
+                    if a == ends[c]:
+                        turn = 0
+                        c += 1
+                        wait = PREF
+                elif a < start + NB:
+                    wait -= 1
+                    if wait == 0:
+                        pe.append(banks[a])
+                        a += 1
+                        wait = PREF
             pe.append(f)
-            name = f[0]
-            if name[0] == "D":
-                n, i = [int(s) for s in name[1:].split(".")]
-            if c < len(CHUNKS) and name[0] == "D" and 4 * n + i >= 4 * starts[c] - LAG:
-                pe += ahead[:2]
-                ahead = ahead[2:]
-                if not ahead:
-                    c += 1
-                    if c < len(CHUNKS):
-                        pe += first_layer[c][:NB]
-                        ahead = first_layer[c][NB:]
+        assert a == 64
 
         weave([sp, act, gp, dve, pe])

@@ -20,19 +20,20 @@ NQ = 8
 H3 = HA - DIN
 DELTA = 2.0 ** -62
 NU = 16
-CHUNKS = (7, 5, 4)
+CHUNKS = (8, 5, 3)
 SECOND = ((), (), (0, 1, 2, 3), (4, 5, 6, 7))
 GUARD = (12, 13, 14, 15)
-EARLY = 14
-STARTS = (12, 43)
+EARLY = 16
+AHEAD = (4, 3)
 RATE0 = (2, 1)
-RATEG = (4, 3)
-RATE = (4, 3)
+RATEG = (2, 1)
+RATE = (3, 2)
 OPOS = 3
 HQD = 3
 RP = 1
-PREF = 3
+PREF = 2
 NB = 4
+NBV = 4
 
 
 def weave(queues):
@@ -69,7 +70,7 @@ def tile_implicitnet_pa_t_kernel(tc, h3, x_in, W4, b4, W5, b5, out):
             return pool.tile(shape, dt, name=tag, tag=tag, bufs=bufs, align_bytes=64)
 
         def bank(tag):
-            return psum.tile([P, 512], F32, name=tag, tag=tag, bufs=NB)
+            return psum.tile([P, 512], F32, name=tag, tag=tag, bufs=NB if tag == "pa" else NBV)
 
         def big(shape, dt):
             return ring(shape, dt, "S", 13)
@@ -553,7 +554,7 @@ def tile_implicitnet_pa_t_kernel(tc, h3, x_in, W4, b4, W5, b5, out):
             k += 4
             if c < len(ends):
                 start = 4 if c == 0 else ends[c - 1]
-                if c == 0 or k >= cfeed + STARTS[c - 1]:
+                if c == 0 or k >= unit_at[sum(CHUNKS[:c]) - AHEAD[c - 1]]:
                     while c and a < start + NB:
                         pe.append(banks[a])
                         a += 1

@@ -418,9 +418,11 @@ def tile_implicitnet_pa_t_kernel(tc, h3, x_in, W4, b4, W5, b5, out):
         add(dve, "W4Q3", ["W4E3"], w4q, 4, 8)
         dve_xe(1, 0)
         dve_xe(1, 1)
+        dve_xq(1)
         for q in range(2, NQ):
             dve_xe(q, 0)
-            dve_xq(q - 1)
+            if q > 2:
+                dve_xq(q - 1)
             dve_xe(q, 1)
         dve_w5e(0)
         dve_xq(NQ - 1)

@@ -31,9 +31,9 @@ RATE = (3, 2)
 OPOS = 3
 HQD = 3
 RP = 1
+NA0 = 5
 PREF = 2
 NB = 4
-NBV = 4
 
 
 def weave(queues):
@@ -69,8 +69,20 @@ def tile_implicitnet_pa_t_kernel(tc, h3, x_in, W4, b4, W5, b5, out):
         def ring(shape, dt, tag, bufs):
             return pool.tile(shape, dt, name=tag, tag=tag, bufs=bufs, align_bytes=64)
 
+        rings = {"pa": [list(range(NA0)), 0], "pv": [list(range(NA0, 8)), 0]}
+
         def bank(tag):
-            return psum.tile([P, 512], F32, name=tag, tag=tag, bufs=NB if tag == "pa" else NBV)
+            r = rings[tag]
+            b = r[0][r[1] % len(r[0])]
+            r[1] += 1
+            return psum.tile([P, 512], F32, name="bank%d" % b, tag="bank%d" % b, bufs=1)
+
+        def even_banks():
+            a, v = rings["pa"], rings["pv"]
+            a[0], a[1] = [a[0][(a[1] + k) % len(a[0])] for k in range(len(a[0]))], 0
+            v[0], v[1] = [v[0][(v[1] + k) % len(v[0])] for k in range(len(v[0]))], 0
+            while len(a[0]) > 4:
+                v[0].append(a[0].pop(0))
 
         def big(shape, dt):
             return ring(shape, dt, "S", 13)
@@ -97,7 +109,6 @@ def tile_implicitnet_pa_t_kernel(tc, h3, x_in, W4, b4, W5, b5, out):
         nc.vector.memset(dl[:], DELTA)
         make_identity(nc, ident[:])
         nc.scalar.dma_start(out=xin[:], in_=x_in.rearrange("(p g) c -> p (g c)", g=NG))
-        nc.scalar.dma_start(out=b4b[:].rearrange("p (g t) -> p g t", g=2), in_=b4.rearrange("(g p t) -> p g t", g=2, t=4))
         nc.scalar.activation(out=warm[:], in_=dl[:], func=FN.Sigmoid)
 
         tiles = {}
@@ -130,10 +141,10 @@ def tile_implicitnet_pa_t_kernel(tc, h3, x_in, W4, b4, W5, b5, out):
         add(sp, "LW0", [], ld_w4, 0)
         add(sp, "LW1", [], ld_w4, 1)
         add(sp, "LX1", [], ld_x, 1)
-        add(sp, "LX2", [], ld_x, 2)
-        add(sp, "LW5", [], ld_w5)
-        for q in range(3, NQ):
+        add(sp, "LB4", [], lambda: nc.sync.dma_start(out=b4b[:].rearrange("p (g t) -> p g t", g=2), in_=b4.rearrange("(g p t) -> p g t", g=2, t=4)))
+        for q in range(2, NQ):
             add(sp, "LX%d" % q, [], ld_x, q)
+        add(sp, "LW5", [], ld_w5)
         add(sp, "B5", [], lambda: nc.sync.dma_start(out=b5bc[:], in_=b5.partition_broadcast(P)))
 
         def run_b4():
@@ -142,7 +153,7 @@ def tile_implicitnet_pa_t_kernel(tc, h3, x_in, W4, b4, W5, b5, out):
             nc.vector.tensor_scalar(out=nb4[:], in0=b4b[:], scalar1=-100.0, scalar2=None, op0=ALU.mult)
 
         def w4t(k):
-            tiles["w4t", k] = pt = bank("pv")
+            tiles["w4t", k] = pt = bank("pa")
             for jj in range(2):
                 for u in range(2):
                     j = 2 * k + jj
@@ -411,10 +422,10 @@ def tile_implicitnet_pa_t_kernel(tc, h3, x_in, W4, b4, W5, b5, out):
 
         dve_xe(0, 0)
         dve_xe(0, 1)
-        add(dve, "B4", [], run_b4)
         dve_xq(0)
         add(dve, "W4Q0", ["W4E0"], w4q, 0, 2)
         add(dve, "W4Q1", ["W4E1"], w4q, 2, 4)
+        add(dve, "B4", ["LB4"], run_b4)
         add(dve, "W4Q3", ["W4E3"], w4q, 4, 8)
         dve_xe(1, 0)
         dve_xe(1, 1)
@@ -567,6 +578,8 @@ def tile_implicitnet_pa_t_kernel(tc, h3, x_in, W4, b4, W5, b5, out):
                         a += 1
                         turn -= rate[1]
                     if a == ends[c]:
+                        if c == 0:
+                            add(pe, "EVEN", [], even_banks)
                         turn = 0
                         c += 1
                         wait = PREF

import math
from contextlib import ExitStack

import concourse.mybir as mybir
from concourse.masks import make_identity

F32 = mybir.dt.float32
BF16 = mybir.dt.bfloat16
U32 = mybir.dt.uint32
U8 = mybir.dt.uint8
FP8X4 = mybir.dt.float8_e4m3fn_x4
ALU = mybir.AluOpType
FN = mybir.ActivationFunctionType

P = 128
N_TOK, HA, HB, HC, DIN = 4096, 512, 1024, 256, 3
FLOPS = 2 * N_TOK * HA * HB + 2 * N_TOK * HB * HC
NG = N_TOK // P
NQ = 8
H3 = HA - DIN
DELTA = 2.0 ** -62
NU = 16
CHUNKS = (8, 5, 3)
SECOND = ((), (), (0, 1, 2, 3), (4, 5, 6, 7))
GUARD = (12, 13, 14, 15)
EARLY = 16
AHEAD = (4, 3)
RATE0 = (2, 1)
RATEG = (2, 1)
RATE = (3, 2)
OPOS = 3
HQD = 3
RP = 1
NA0 = 5
PREF = 2
NB = 4


def weave(queues):
    done = set()
    heads = [0 for q in queues]
    left = sum(len(q) for q in queues)
    while left:
        before = left
        for i, q in enumerate(queues):
            if heads[i] < len(q):
                name, needs, run = q[heads[i]]
                if all(n in done for n in needs):
                    run()
                    done.add(name)
                    heads[i] += 1
                    left -= 1
        assert left < before, "the queues wait for each other"


def tile_implicitnet_pa_t_kernel(tc, h3, x_in, W4, b4, W5, b5, out):
    nc = tc.nc
    h3v = h3.rearrange("(p g) k -> p g k", g=NG)
    outv = out.rearrange("(p g) n -> p g n", g=NG)

    with ExitStack() as ctx:
        pool = ctx.enter_context(tc.tile_pool(name="sb", bufs=1))
        psum = ctx.enter_context(tc.psum_pool(name="psum", bufs=1))
        ctx.enter_context(tc.manual_schedule())

        def keep(shape, dt, name):
            return pool.tile(shape, dt, name=name, align_bytes=64)

        def ring(shape, dt, tag, bufs):
            return pool.tile(shape, dt, name=tag, tag=tag, bufs=bufs, align_bytes=64)

        rings = {"pa": [list(range(NA0)), 0], "pv": [list(range(NA0, 8)), 0]}

        def bank(tag):
            r = rings[tag]
            b = r[0][r[1] % len(r[0])]
            r[1] += 1
            return psum.tile([P, 512], F32, name="bank%d" % b, tag="bank%d" % b, bufs=1)

        def even_banks():
            a, v = rings["pa"], rings["pv"]
            a[0], a[1] = [a[0][(a[1] + k) % len(a[0])] for k in range(len(a[0]))], 0
            v[0], v[1] = [v[0][(v[1] + k) % len(v[0])] for k in range(len(v[0]))], 0
            while len(a[0]) > 4:
                v[0].append(a[0].pop(0))

        def big(shape, dt):
            return ring(shape, dt, "S", 13)

        ident = keep([P, P], F32, "ident")
        dl = keep([P, 1], F32, "dl")
        warm = keep([P, 1], F32, "warm")
        b4b = keep([P, 8], BF16, "b4b")
        b4f = keep([P, 8], F32, "b4f")
        pb4 = keep([P, 8], F32, "pb4")
        nb4 = keep([P, 8], F32, "nb4")
        b5bc = keep([P, HC], BF16, "b5bc")
        xin = keep([P, NG * DIN], BF16, "xin")
        X = []
        for q in range(NQ):
            X.append(ring([P, 4, HA], BF16, "X", NQ))
        xc = [keep([P, 512], U32, "xc%d" % q) for q in range(NQ)]
        xs = [keep([P, 512], U8, "xs%d" % q) for q in range(NQ)]
        w4c = keep([P, HB], U32, "w4c")
        w4s = keep([P, HB], U8, "w4s")
        w5c = keep([P, 512], U32, "w5c")
        w5s = keep([P, 512], U8, "w5s")

        nc.vector.memset(dl[:], DELTA)
        make_identity(nc, ident[:])
        nc.scalar.dma_start(out=xin[:], in_=x_in.rearrange("(p g) c -> p (g c)", g=NG))
        nc.scalar.activation(out=warm[:], in_=dl[:], func=FN.Sigmoid)

        tiles = {}

        def words(t):
            return t[:].bitcast(F32)

        def mx(o, lw, ls, rw, rs, start, stop):
            nc.tensor.matmul_mx(out=o, lhsT=lw.bitcast(FP8X4), lhsT_scale=ls, rhs=rw.bitcast(FP8X4), rhs_scale=rs, start=start, stop=stop)

        sp, act, gp, dve, pe = [], [], [], [], []
        feeds = []

        def add(queue, name, needs, run, *args):
            queue.append((name, needs, lambda: run(*args)))

        def ld_x(q):
            nc.sync.dma_start(out=X[q][:, :, 0:H3], in_=h3v[:, 4 * q : 4 * q + 4, :])

        def ld_w4(h):
            if h == 0:
                tiles["w4"] = big([P, 8 * HA], BF16)
            nc.sync.dma_start(out=tiles["w4"][:, 2048 * h : 2048 * h + 2048], in_=W4.rearrange("(g m t) k -> m g (t k)", g=2, t=4)[:, h, :])

        def ld_w5():
            tiles["w5"] = big([P, 2 * HB], BF16)
            nc.sync.dma_start(out=tiles["w5"][:].rearrange("p (a k) -> p a k", a=2), in_=W5.rearrange("(a n) k -> n a k", a=2))

        add(sp, "LX0", [], ld_x, 0)
        add(sp, "LW0", [], ld_w4, 0)
        add(sp, "LW1", [], ld_w4, 1)
        add(sp, "LX1", [], ld_x, 1)
        add(sp, "LB4", [], lambda: nc.sync.dma_start(out=b4b[:].rearrange("p (g t) -> p g t", g=2), in_=b4.rearrange("(g p t) -> p g t", g=2, t=4)))
        for q in range(2, NQ):
            add(sp, "LX%d" % q, [], ld_x, q)
        add(sp, "LW5", [], ld_w5)
        add(sp, "B5", [], lambda: nc.sync.dma_start(out=b5bc[:], in_=b5.partition_broadcast(P)))

        def run_b4():
            nc.vector.tensor_copy(out=b4f[:], in_=b4b[:])
            nc.vector.tensor_scalar(out=pb4[:], in0=b4b[:], scalar1=100.0, scalar2=None, op0=ALU.mult)
            nc.vector.tensor_scalar(out=nb4[:], in0=b4b[:], scalar1=-100.0, scalar2=None, op0=ALU.mult)

        def w4t(k):
            tiles["w4t", k] = pt = bank("pa")
            for jj in range(2):
                for u in range(2):
                    j = 2 * k + jj
                    nc.tensor.transpose(pt[:, 256 * jj + 128 * u : 256 * jj + 128 * u + 128], words(tiles["w4"])[:, 256 * j + 128 * u : 256 * j + 128 * u + 128], ident[:])

        def w4e(k):
            if k == 0:
                tiles["w4g"] = big([P, 8 * HA], BF16)
            nc.scalar.copy(
                out=words(tiles["w4g"]).rearrange("p (j m u) -> p j m u", j=8, u=2)[:, 2 * k : 2 * k + 2],
                in_=tiles["w4t", k][:].rearrange("p (j u m) -> p j m u", j=2, u=2),
            )

        def w4q(lo, hi):
            nc.vector.quantize_mx(out=w4c[:, 128 * lo : 128 * hi].bitcast(FP8X4), scales=w4s[:, 128 * lo : 128 * hi], in_=tiles["w4g"][:, 512 * lo : 512 * hi])

        def w5t(g):
            tiles["w5t", g] = pt = bank("pv")
            for a in range(2):
                for u in range(2):
                    lo = 512 * a + 256 * g + u
                    nc.tensor.transpose(pt[:, 256 * a + 128 * u : 256 * a + 128 * u + 128], words(tiles["w5"])[:, lo : lo + 255 : 2], ident[:])

        def w5e(g):
            if g == 0:
                tiles["w5g"] = big([P, 2 * HB], BF16)
            nc.vector.tensor_copy(
                out=words(tiles["w5g"]).rearrange("p (g a n u) -> p g a n u", g=2, a=2, u=2)[:, g],
                in_=tiles["w5t", g][:].rearrange("p (a u n) -> p a n u", a=2, u=2),
            )

        def w5q():
            nc.vector.quantize_mx(out=w5c[:].bitcast(FP8X4), scales=w5s[:], in_=tiles["w5g"][:])

        def xcat(q):
            last = X[q][:, :, H3 - 1 : H3]
            nc.gpsimd.tensor_copy(out=last, in_=last)
            nc.gpsimd.tensor_copy(out=X[q][:, :, H3:HA], in_=xin[:].rearrange("p (g c) -> p g c", c=DIN)[:, 4 * q : 4 * q + 4, :])

        def xt(q, b):
            tiles["xt", q, b] = pt = bank("pv")
            xw = X[q][:].rearrange("p g k -> p (g k)").bitcast(F32)
            for ii in range(2):
                for u in range(2):
                    lo = 256 * (2 * b + ii) + 128 * u
                    nc.tensor.transpose(pt[:, 256 * u + 128 * ii : 256 * u + 128 * ii + 128], xw[:, lo : lo + 128], ident[:])

        def xe(q, b):
            if b == 0:
                tiles["xg", q] = ring([P, 2048], BF16, "xg", 2)
            nc.vector.tensor_scalar(
                out=tiles["xg", q][:, 1024 * b : 1024 * b + 1024].rearrange("p (x u e) -> p x u e", u=2, e=2),
                in0=tiles["xt", q, b][:].bitcast(BF16).rearrange("p (u x e) -> p x u e", u=2, e=2),
                scalar1=math.sqrt(0.5), scalar2=None, op0=ALU.mult,
            )

        def xq(q):
            nc.vector.quantize_mx(out=xc[q][:].bitcast(FP8X4), scales=xs[q][:], in_=tiles["xg", q][:])

        def l1a(n, t):
            q, j = n // 2, 4 * (n % 2) + t
            tiles["a", n, t] = pa = bank("pa")
            mx(pa[:], w4c[:, 128 * j : 128 * j + 128], w4s[:, 128 * j : 128 * j + 128], xc[q][:], xs[q][:], True, True)

        def sig1(n, t):
            j = 4 * (n % 2) + t
            if t == 0:
                tiles["S", n] = big([P, 4, 512], F32)
            bias, scale = (pb4, 100.0) if n not in GUARD else (nb4, -100.0)
            nc.scalar.activation(out=tiles["S", n][:, t, :], in_=tiles["a", n, t][:], func=FN.Sigmoid, bias=bias[:, j : j + 1], scale=scale)

        def ln1(n):
            s = tiles["S", n][:].rearrange("p t x -> p (t x)")
            nc.scalar.activation(out=s, in_=s, func=FN.Ln, bias=dl[:], scale=1.0)

        def htile(n):
            if ("H", n // 2) not in tiles:
                tiles["H", n // 2] = ring([P, 2, 2048], BF16, "H", 2)
            return tiles["H", n // 2][:, n % 2, :]

        def hview(n):
            return tiles["H", n // 2][:, n % 2, :]

        def base(n, t):
            j = 4 * (n % 2) + t
            if t == 0:
                nc.gpsimd.memset(htile(n)[:, 0:2], 0.0)
            s = tiles["S", n][:, t, :]
            nc.gpsimd.tensor_scalar(out=s, in0=s, scalar1=-0.01, scalar2=b4f[:, j : j + 1], op0=ALU.mult, op1=ALU.add)

        def l1d(n, i):
            q, g = n // 2, n % 2
            tiles["d", n, i] = pd = bank("pv")
            for t in range(4):
                j = 4 * g + t
                mx(pd[:, 128 * t : 128 * t + 128], w4c[:, 128 * j : 128 * j + 128], w4s[:, 128 * j : 128 * j + 128], xc[q][:, 128 * i : 128 * i + 128], xs[q][:, 128 * i : 128 * i + 128], True, True)

        def hsum(n, i):
            nc.vector.tensor_tensor(
                out=hview(n)[:, 512 * i : 512 * i + 512].rearrange("p (c s t) -> p c t s", s=4, t=4),
                in0=tiles["d", n, i][:].rearrange("p (t c s) -> p c t s", t=4, s=4),
                in1=tiles["S", n][:, :, 128 * i : 128 * i + 128].rearrange("p t (c s) -> p c t s", s=4),
                op=ALU.add,
            )

        def hrelu(n, lo, hi):
            h = hview(n)[:, 4 * lo : 4 * hi]
            nc.vector.tensor_scalar(out=h, in0=h, scalar1=0.0, scalar2=None, op0=ALU.max)

        def guard(n, i):
            g = n % 2
            if i == 0:
                tiles["G", n] = ring([P, 2048], BF16, "X", NQ)
            nc.vector.tensor_tensor(
                out=tiles["G", n][:].rearrange("p (i r t) -> p i r t", i=4, t=4)[:, i],
                in0=tiles["d", n, i][:].rearrange("p (t r) -> p r t", t=4),
                in1=b4f[:, 4 * g : 4 * g + 4].unsqueeze(1).to_broadcast([P, P, 4]),
                op=ALU.add,
            )

        def hrelu2(q):
            h = tiles["H", q][:].rearrange("p g x -> p (g x)")
            nc.vector.tensor_scalar(out=h, in0=h, scalar1=0.0, scalar2=None, op0=ALU.max)

        def hnone():
            pass

        def hscale(n, lo, hi):
            h = htile(n) if lo == 0 else hview(n)
            nc.vector.tensor_scalar(
                out=h[:, 4 * lo : 4 * hi].rearrange("p (c s t) -> p c t s", s=4, t=4),
                in0=tiles["S", n][:, :, lo:hi].rearrange("p t (c s) -> p c t s", s=4),
                scalar1=-0.01, scalar2=None, op0=ALU.mult,
            )

        def hmax(n, lo, hi):
            h = hview(n)[:, 4 * lo : 4 * hi]
            nc.vector.tensor_tensor(out=h, in0=h, in1=tiles["G", n][:, 4 * lo : 4 * hi], op=ALU.max)

        def hquant(q, g0, g1, lo, hi):
            if g0 == 0 and lo == 0:
                tiles["Hc", q] = ring([P, 2, 512], U32, "Hc", 2)
                tiles["Hs", q] = ring([P, 2, 512], U8, "Hs", 2)
            if g1 - g0 == 2:
                nc.vector.quantize_mx(
                    out=tiles["Hc", q][:].rearrange("p g x -> p (g x)").bitcast(FP8X4),
                    scales=tiles["Hs", q][:].rearrange("p g x -> p (g x)"),
                    in_=tiles["H", q][:].rearrange("p g x -> p (g x)"),
                )
            else:
                nc.vector.quantize_mx(out=tiles["Hc", q][:, g0, lo:hi].bitcast(FP8X4), scales=tiles["Hs", q][:, g0, lo:hi], in_=tiles["H", q][:, g0, 4 * lo : 4 * hi])

        def l2(q, b):
            tiles["o", q, b] = po = bank("pv")
            hc, hs = tiles["Hc", q], tiles["Hs", q]
            for ii in range(2):
                i = 2 * b + ii
                for g in range(2):
                    mx(po[:, 256 * ii : 256 * ii + 256], hc[:, g, 128 * i : 128 * i + 128], hs[:, g, 128 * i : 128 * i + 128], w5c[:, 256 * g : 256 * g + 256], w5s[:, 256 * g : 256 * g + 256], g == 0, g == 1)

        def oe(q, b):
            if b == 0:
                tiles["v", q] = ring([P, 4, HC], F32, "v", 8)
            nc.vector.tensor_tensor(
                out=tiles["v", q][:, 2 * b : 2 * b + 2, :],
                in0=tiles["o", q, b][:].rearrange("p (i n) -> p i n", i=2),
                in1=b5bc[:].unsqueeze(1).to_broadcast([P, 2, HC]),
                op=ALU.add,
            )

        def sig2(q, lo, hi):
            if lo == 0:
                tiles["s2", q] = big([P, 4, HC], F32)
            nc.scalar.activation(out=tiles["s2", q][:, lo:hi, :], in_=tiles["v", q][:, lo:hi, :], func=FN.Sigmoid, scale=-100.0)

        def ln2(q, lo, hi):
            s = tiles["s2", q][:, lo:hi, :]
            nc.scalar.activation(out=s, in_=s, func=FN.Ln, bias=dl[:], scale=1.0)

        def fin2(q, lo, hi):
            s = tiles["s2", q][:, lo:hi, :]
            nc.vector.scalar_tensor_tensor(out=s, in0=s, scalar=-0.01, in1=tiles["v", q][:, lo:hi, :], op0=ALU.mult, op1=ALU.max)

        def store(q, lo, hi):
            nc.sync.dma_start(out=outv[:, 4 * q + lo : 4 * q + hi, :], in_=tiles["s2", q][:, lo:hi, :])

        def parts(q):
            return ((0, 2), (2, 4)) if q == NQ - 1 else ((0, 4),)

        for k in range(4):
            add(act, "W4E%d" % k, ["W4T%d" % k], w4e, k)

        def act_sig1(n):
            for t in range(4):
                add(act, "S%d.%d" % (n, t), ["A%d.%d" % (n, t), "B4"], sig1, n, t)

        def act_ln1(n):
            add(act, "L%d" % n, ["S%d.3" % n], ln1, n)

        def act_sig2(q):
            for lo, hi in parts(q):
                add(act, "S2_%d.%d" % (q, hi), ["OE%d.%d" % (q, hi // 2 - 1)], sig2, q, lo, hi)

        def act_ln2(q):
            for lo, hi in parts(q):
                add(act, "L2_%d.%d" % (q, hi), ["S2_%d.%d" % (q, hi)], ln2, q, lo, hi)

        first = 0
        for c, size in enumerate(CHUNKS + (0,)):
            units = range(first, first + size)
            first += size
            for n in units:
                act_sig1(n)
            for q in SECOND[c]:
                act_sig2(q)
            for n in units:
                act_ln1(n)
            for q in SECOND[c]:
                act_ln2(q)
        second = [q for c in SECOND for q in c]

        for q in range(NQ):
            add(gp, "XC%d" % q, ["LX%d" % q], xcat, q)
        for n in range(NU):
            if n in GUARD:
                continue
            for t in range(4):
                add(gp, "P%d.%d" % (n, t), ["L%d" % n, "B4"], base, n, t)

        def dve_xe(q, b):
            add(feeds, "T%d.%d" % (q, b), ["XC%d" % q], xt, q, b)
            add(dve, "XE%d.%d" % (q, b), ["T%d.%d" % (q, b)], xe, q, b)

        def dve_xq(q):
            add(dve, "XQ%d" % q, ["XE%d.1" % q], xq, q)

        def dve_hq2(q):
            add(dve, "HQ%d" % q, ["R%d.512" % (2 * q + 1), "R%d.512" % (2 * q)], hquant, q, 0, 2, 0, 512)

        def dve_hq1(n, lo=0, hi=512):
            add(dve, "HQ%d.%d" % (n, hi), ["R%d.%d" % (n, hi)], hquant, n // 2, n % 2, n % 2 + 1, lo, hi)

        def dve_scale(n, lo=0, hi=512):
            add(dve, "M%d.%d" % (n, hi), ["L%d" % n], hscale, n, lo, hi)

        def dve_max(n, lo=0, hi=512):
            add(dve, "R%d.%d" % (n, hi), ["M%d.%d" % (n, hi), "G%d.3" % n], hmax, n, lo, hi)

        def dve_w5e(g):
            add(feeds, "W5T%d" % g, ["LW5"], w5t, g)
            add(dve, "W5E%d" % g, ["W5T%d" % g], w5e, g)

        def dve_oe(k):
            q, b = k // 2, k % 2
            add(feeds, "O%d.%d" % (q, b), ["HQ15.%d" % (256 * (b + 1)) if q == NQ - 1 else "HQ%d" % q, "W5Q"], l2, q, b)
            add(dve, "OE%d.%d" % (q, b), ["O%d.%d" % (q, b), "B5"], oe, q, b)

        def dve_f2(q):
            for lo, hi in parts(q):
                add(dve, "F2_%d.%d" % (q, hi), ["L2_%d.%d" % (q, hi)], fin2, q, lo, hi)

        def dve_guard(k):
            n, i = GUARD[k // 4], k % 4
            add(feeds, "D%d.%d" % (n, i), ["XQ%d" % (n // 2), "W4Q%d" % (3 if n % 2 else 1)], l1d, n, i)
            add(dve, "G%d.%d" % (n, i), ["D%d.%d" % (n, i)], guard, n, i)

        dve_xe(0, 0)
        dve_xe(0, 1)
        dve_xq(0)
        add(dve, "W4Q0", ["W4E0"], w4q, 0, 2)
        add(dve, "W4Q1", ["W4E1"], w4q, 2, 4)
        add(dve, "B4", ["LB4"], run_b4)
        add(dve, "W4Q3", ["W4E3"], w4q, 4, 8)
        dve_xe(1, 0)
        dve_xe(1, 1)
        dve_xq(1)
        for q in range(2, NQ):
            dve_xe(q, 0)
            if q > 2:
                dve_xq(q - 1)
            dve_xe(q, 1)
        dve_w5e(0)
        dve_xq(NQ - 1)
        dve_w5e(1)
        prep = len(feeds)
        guards = 4 * len(GUARD)
        for k in range(EARLY):
            dve_guard(k)
        add(dve, "W5Q", ["W5E1"], w5q)
        state = {"g": EARLY, "o": 0}
        cfeed = len(feeds)

        pend = []

        def hq_now():
            while pend:
                dve_hq2(pend.pop(0))

        def flush(n):
            for c in range(1, len(CHUNKS)):
                if CHUNKS[c] and n == sum(CHUNKS[:c]):
                    for q in SECOND[c]:
                        hq_now()
                        while state["o"] < 2 * q + 2:
                            dve_oe(state["o"])
                            state["o"] += 1

        def some_oe(n, done):
            if state["o"] < 14 and state["o"] // 2 < done:
                dve_oe(state["o"])
                state["o"] += 1

        def some_guard(n):
            left = sum(1 for m in range(n, NU) if m not in GUARD and m < GUARD[-1])
            more = guards - state["g"] if left < 2 else (guards - state["g"]) // left
            if n < GUARD[0]:
                for k in range(state["g"], state["g"] + more):
                    dve_guard(k)
                state["g"] += more

        def dve_c(n, i):
            add(feeds, "D%d.%d" % (n, i), ["XQ%d" % (n // 2), "W4Q%d" % (3 if n % 2 else 1)], l1d, n, i)
            add(dve, "C%d.%d" % (n, i), ["D%d.%d" % (n, i), "P%d.3" % n], hsum, n, i)

        def dve_relu(n, lo, hi):
            add(dve, "R%d.%d" % (n, hi), ["C%d.%d" % (n, hi // 128 - 1)], hrelu, n, lo, hi)

        done = 0
        unit_at = {}
        for n in range(NU - 1):
            flush(n)
            unit_at[n] = len(feeds)
            if n in GUARD:
                if state["g"] < 4 * GUARD.index(n) + 4:
                    for k in range(state["g"], 4 * GUARD.index(n) + 4):
                        dve_guard(k)
                    state["g"] = 4 * GUARD.index(n) + 4
                dve_scale(n)
                some_oe(n, done)
                if pend:
                    hq_now()
                    done += 1
                dve_max(n)
            else:
                for i in range(4):
                    dve_c(n, i)
                    if i == OPOS:
                        some_oe(n, done)
                    if i == HQD and pend:
                        hq_now()
                        done += 1
                some_guard(n)
                if RP and n < 14 and n // 2 * 2 not in GUARD and n // 2 * 2 + 1 not in GUARD:
                    if n % 2:
                        add(dve, "R%d.512" % n, ["C%d.3" % n, "C%d.3" % (n - 1)], hrelu2, n // 2)
                        add(dve, "R%d.512" % (n - 1), [], hnone)
                else:
                    dve_relu(n, 0, 512)
            if n % 2:
                pend.append(n // 2)
        hq_now()
        if 15 in GUARD:
            dve_scale(15, 0, 256)
            dve_hq1(14)
            dve_max(15, 0, 256)
            dve_scale(15, 256, 512)
            dve_hq1(15, 0, 256)
            while state["o"] < 13:
                dve_oe(state["o"])
                state["o"] += 1
            dve_max(15, 256, 512)
        else:
            dve_c(15, 0)
            dve_c(15, 1)
            dve_hq1(14)
            dve_relu(15, 0, 256)
            dve_c(15, 2)
            dve_hq1(15, 0, 256)
            dve_c(15, 3)
            while state["o"] < 13:
                dve_oe(state["o"])
                state["o"] += 1
            dve_relu(15, 256, 512)
        dve_oe(13)
        dve_hq1(15, 256, 512)
        dve_oe(14)
        dve_f2(second[0])
        dve_oe(15)
        for q in second[1:]:
            dve_f2(q)
        for q in second:
            for lo, hi in parts(q):
                add(sp, "ST%d.%d" % (q, hi), ["F2_%d.%d" % (q, hi)], store, q, lo, hi)

        banks = []
        for n in range(NU):
            for t in range(4):
                add(banks, "A%d.%d" % (n, t), ["XQ%d" % (n // 2), "W4Q%d" % (3 if n % 2 else t // 2)], l1a, n, t)
        pe += feeds[:2]
        for k in (0, 1):
            add(pe, "W4T%d" % k, ["LW0"], w4t, k)
        for k in (2, 3):
            add(pe, "W4T%d" % k, ["LW1"], w4t, k)
        pe += banks[:2] + feeds[2:3] + banks[2:4] + feeds[3:4]
        ends = [4 * sum(CHUNKS[: c + 1]) for c in range(len(CHUNKS)) if CHUNKS[c]]
        c = 0
        a = 4
        turn = 0
        wait = 0
        for k, f in enumerate(feeds[4:]):
            k += 4
            if c < len(ends):
                start = 4 if c == 0 else ends[c - 1]
                if c == 0 or k >= unit_at[sum(CHUNKS[:c]) - AHEAD[c - 1]]:
                    while c and a < start + NB:
                        pe.append(banks[a])
                        a += 1
                    rate = (RATE0 if k < prep else RATEG) if c == 0 else RATE
                    turn += rate[0]
                    while turn >= rate[1] and a < ends[c]:
                        pe.append(banks[a])
                        a += 1
                        turn -= rate[1]
                    if a == ends[c]:
                        if c == 0:
                            add(pe, "EVEN", [], even_banks)
                        turn = 0
                        c += 1
                        wait = PREF
                elif a < start + NB:
                    wait -= 1
                    if wait == 0:
                        pe.append(banks[a])
                        a += 1
                        wait = PREF
            pe.append(f)
        assert a == 64

        weave([sp, act, gp, dve, pe])
